import numpy as np
import ml_dtypes


def mxq(x, axis, fmt="e4m3"):
    dtype, down = {"e4m3": (ml_dtypes.float8_e4m3fn, 7), "e5m2": (ml_dtypes.float8_e5m2, 14)}[fmt]
    v = np.moveaxis(np.asarray(x, np.float32).astype(ml_dtypes.bfloat16).astype(np.float64), axis, -1)
    blocks = v.reshape(v.shape[:-1] + (-1, 32))
    amax = np.abs(blocks).max(-1, keepdims=True)
    byte = np.maximum(np.where(amax > 0, np.frexp(amax)[1] - 1 + 127, 0) - down, 1)
    scale = np.exp2(byte - 127.0)
    codes = (blocks / scale).astype(np.float32).astype(dtype).astype(np.float64)
    return np.moveaxis((codes * scale).reshape(v.shape), -1, axis)


WIDE = False


def mx_kscale(k):
    if not WIDE:
        return np.ones(k)
    levels = np.array([10, -10, 5, -5, 0])
    if k % 512:
        return np.exp2(np.random.permutation(np.resize(levels, k // 32))).repeat(32)
    a = np.empty((k // 512, 16))
    for p in range(k // 512):
        a[p, :8] = np.random.permutation(np.resize(levels, 8))
        for g in range(8):
            far = levels[np.abs(levels - a[p, g]) >= 10]
            a[p, g + 8] = far[np.random.randint(len(far))]
    return np.exp2(a.ravel()).repeat(32)


BF16 = ml_dtypes.bfloat16


def bf(x):
    return np.asarray(x, np.float32).astype(BF16)


def f64(x):
    return np.asarray(x).astype(np.float64)


B, DA, DB, DC, OUT, NS = 4096, 512, 512, 1024, 128, 3
EPS = 1e-5
STREAMS = (("a", DA), ("b", DB), ("c", DC))


def layer_norm(x, w, b):
    mu = x.mean(-1, keepdims=True)
    var = np.square(x - mu).mean(-1, keepdims=True)
    return (x - mu) / np.sqrt(var + EPS) * w + b


def setup_inputs():
    inp = {}
    for name, d in STREAMS:
        t = mx_kscale(d)
        loud = np.exp2(-np.random.uniform(0.0, 8.0, (B, 1)))
        inp["x_" + name] = bf((np.random.standard_normal((B, d)) + 0.5 * np.random.standard_normal((B, 1))) * loud)
        inp["ln_w_" + name] = bf((1.0 + 0.1 * np.random.standard_normal(d)) * t)
        inp["ln_b_" + name] = bf(0.1 * np.random.standard_normal(d) * t)
        inp["W_" + name] = bf(np.random.standard_normal((d, OUT)) / np.sqrt(d) / t[:, None])
        inp["b_" + name] = bf(0.2 * np.random.standard_normal(OUT))
        inp["Wg_" + name] = bf(np.random.standard_normal((d, NS * OUT)) / np.sqrt(d) / t[:, None])
        inp["bg_" + name] = bf(0.2 * np.random.standard_normal(NS * OUT))
    return inp


def reference(x_a, ln_w_a, ln_b_a, W_a, b_a, Wg_a, bg_a,
              x_b, ln_w_b, ln_b_b, W_b, b_b, Wg_b, bg_b,
              x_c, ln_w_c, ln_b_c, W_c, b_c, Wg_c, bg_c):
    streams = ((x_a, ln_w_a, ln_b_a, W_a, b_a, Wg_a, bg_a),
               (x_b, ln_w_b, ln_b_b, W_b, b_b, Wg_b, bg_b),
               (x_c, ln_w_c, ln_b_c, W_c, b_c, Wg_c, bg_c))
    gate_logits = 0.0
    outputs = []
    for x, lw, lb, W, b, Wg, bg in streams:
        f = np.maximum(layer_norm(f64(x), f64(lw), f64(lb)), 0.0)
        fq = mxq(f, 1, "e4m3")
        outputs.append((fq @ mxq(f64(W), 0, "e4m3")) + f64(b))
        gate_logits = gate_logits + ((fq @ mxq(f64(Wg), 0, "e4m3")) + f64(bg))
    g = gate_logits.reshape(B, NS, OUT)
    e = np.exp(g - g.max(1, keepdims=True))
    gate = e / e.sum(1, keepdims=True)
    return sum(gate[:, i] * outputs[i] for i in range(NS))

@@ -1,0 +1,406 @@
+from contextlib import ExitStack
+
+import concourse.mybir as mybir
+from concourse.masks import make_identity
+
+F32 = mybir.dt.float32
+BF16 = mybir.dt.bfloat16
+U32 = mybir.dt.uint32
+U8 = mybir.dt.uint8
+FP8X4 = mybir.dt.float8_e4m3fn_x4
+ALU = mybir.AluOpType
+ACT = mybir.ActivationFunctionType
+
+P = 128
+PACK = 4
+K_PASS = P * PACK
+ROWS = 4096
+BLOCK = 512
+ROW_TILES = BLOCK // P
+N_BLOCKS = ROWS // BLOCK
+OUT = 128
+NS = 3
+K_ALL = 2048
+PASSES = K_ALL // K_PASS
+STREAM_OF_PASS = (0, 1, 2, 2)
+PASSES_OF_STREAM = ((0,), (1,), (2, 3))
+W_COLS = OUT + NS * OUT
+LAST_GATE_COL = W_COLS - OUT
+EPS = 1e-5
+VECTOR_ROW_TILES = 1
+
+OUT_BIAS_ROW = 0
+GATE_BIAS_ROW = OUT_BIAS_ROW + NS
+PARAM_ROWS = GATE_BIAS_ROW + NS * NS
+
+LN_SLOT = 16
+
+FLOPS = 2 * ROWS * K_ALL * W_COLS
+
+STEPS_PER_BLOCK = PASSES
+NORM_LAG = 3
+TRANSPOSE_LAG = NORM_LAG + 1
+REGROUP_LAG = TRANSPOSE_LAG + 1
+QUANT_LAG = REGROUP_LAG + 1
+MERGE_LAG = QUANT_LAG + STEPS_PER_BLOCK
+N_STEPS = N_BLOCKS * STEPS_PER_BLOCK + MERGE_LAG
+
+
+def regroup(nc, grouped, planes):
+    nc.vector.tensor_copy(
+        out=grouped.rearrange("p (c i) t -> p c t i", i=4),
+        in_=planes.rearrange("p t (c i) -> p c t i", i=4),
+    )
+
+
+def tile_vectormerge_pa_t_kernel(
+    tc,
+    x_a, ln_w_a, ln_b_a, W_a, b_a, Wg_a, bg_a,
+    x_b, ln_w_b, ln_b_b, W_b, b_b, Wg_b, bg_b,
+    x_c, ln_w_c, ln_b_c, W_c, b_c, Wg_c, bg_c,
+    out,
+):
+    nc = tc.nc
+    xs = (x_a, x_b, x_c)
+    ln_ws = (ln_w_a, ln_w_b, ln_w_c)
+    ln_bs = (ln_b_a, ln_b_b, ln_b_c)
+    Ws = (W_a, W_b, W_c)
+    bs = (b_a, b_b, b_c)
+    Wgs = (Wg_a, Wg_b, Wg_c)
+    bgs = (bg_a, bg_b, bg_c)
+
+    with ExitStack() as ctx:
+        keep = ctx.enter_context(tc.tile_pool(name="keep", bufs=1))
+        x_pool = ctx.enter_context(tc.tile_pool(name="x_pool", bufs=3))
+        stat_pool = ctx.enter_context(tc.tile_pool(name="stat_pool", bufs=6))
+        norm_pool = ctx.enter_context(tc.tile_pool(name="norm_pool", bufs=4))
+        plane_pool = ctx.enter_context(tc.tile_pool(name="plane_pool", bufs=3))
+        f_pool = ctx.enter_context(tc.tile_pool(name="f_pool", bufs=2))
+        code_pool = ctx.enter_context(tc.tile_pool(name="code_pool", bufs=2))
+        gate_pool = ctx.enter_context(tc.tile_pool(name="gate_pool", bufs=1))
+        out_pool = ctx.enter_context(tc.tile_pool(name="out_pool", bufs=2))
+        psum_xt = ctx.enter_context(tc.psum_pool(name="psum_xt", bufs=3))
+        psum_mx = ctx.enter_context(tc.psum_pool(name="psum_mx", bufs=1))
+        psum_sn = ctx.enter_context(tc.psum_pool(name="psum_sn", bufs=1))
+
+        ctx.enter_context(tc.manual_schedule())
+
+        ident_f32 = keep.tile([P, P], F32)
+        make_identity(nc, ident_f32[:])
+        ident_bf16 = keep.tile([P, P], BF16)
+        make_identity(nc, ident_bf16[:])
+        minus_half = keep.tile([P, ROW_TILES], F32)
+        nc.vector.memset(minus_half[:], -0.5)
+        param_rows = keep.tile([P, P], BF16)
+        nc.vector.memset(param_rows[:], 0.0)
+        param = keep.tile([P, P], F32)
+        ln_raw = keep.tile([P, 2, NS, LN_SLOT], BF16)
+        ln_param = keep.tile([P, 2, PASSES, PACK], F32)
+        gate_bias = keep.tile([P, NS], F32)
+        diff_bias = keep.tile([P, NS - 1], F32)
+        w_raw = keep.tile([P, PASSES, PACK, W_COLS], BF16)
+        w_grouped = keep.tile([P, PASSES, W_COLS, PACK], BF16, align_bytes=64)
+        w_codes = keep.tile([P, PASSES, W_COLS], U32, align_bytes=64)
+        w_scales = keep.tile([P, PASSES, W_COLS], U8, align_bytes=64)
+
+        def load_small_vectors():
+            for s in range(NS):
+                count = len(PASSES_OF_STREAM[s]) * PACK
+                for i, vec in enumerate((ln_ws[s], ln_bs[s])):
+                    nc.sync.dma_start(
+                        out=ln_raw[:, i, s, 0:count].rearrange("p (g j) -> p g j", j=PACK),
+                        in_=vec.rearrange("(g p j) -> p g j", p=P, j=PACK),
+                    )
+                nc.sync.dma_start(
+                    out=param_rows[OUT_BIAS_ROW + s : OUT_BIAS_ROW + s + 1, :],
+                    in_=bs[s].rearrange("(c p) -> c p", p=P),
+                )
+                nc.sync.dma_start(
+                    out=param_rows[GATE_BIAS_ROW + NS * s : GATE_BIAS_ROW + NS * (s + 1), :],
+                    in_=bgs[s].rearrange("(c p) -> c p", p=P),
+                )
+            param_ps = psum_xt.tile([P, P], BF16, tag="xt")
+            nc.tensor.transpose(param_ps[:], param_rows[:], ident_bf16[:])
+            nc.scalar.copy(out=param[:], in_=param_ps[:])
+            for s in range(NS):
+                g0 = PASSES_OF_STREAM[s][0]
+                g1 = PASSES_OF_STREAM[s][-1] + 1
+                nc.scalar.copy(
+                    out=ln_param[:, :, g0:g1, :].rearrange("p i g j -> p i (g j)"),
+                    in_=ln_raw[:, :, s, 0 : (g1 - g0) * PACK],
+                )
+            nc.gpsimd.tensor_add(
+                out=gate_bias[:],
+                in0=param[:, GATE_BIAS_ROW : GATE_BIAS_ROW + NS],
+                in1=param[:, GATE_BIAS_ROW + NS : GATE_BIAS_ROW + 2 * NS],
+            )
+            nc.gpsimd.tensor_add(
+                out=gate_bias[:],
+                in0=gate_bias[:],
+                in1=param[:, GATE_BIAS_ROW + 2 * NS : GATE_BIAS_ROW + 3 * NS],
+            )
+            for i in range(NS - 1):
+                nc.gpsimd.tensor_sub(
+                    out=diff_bias[:, i : i + 1], in0=gate_bias[:, i : i + 1],
+                    in1=gate_bias[:, NS - 1 : NS],
+                )
+
+        def load_weights():
+            for g in range(PASSES):
+                s = STREAM_OF_PASS[g]
+                r0 = (g - PASSES_OF_STREAM[s][0]) * K_PASS
+                rows = slice(r0, r0 + K_PASS)
+                nc.sync.dma_start(
+                    out=w_raw[:, g, :, 0:OUT],
+                    in_=Ws[s][rows, :].rearrange("(p t) n -> p t n", t=PACK),
+                )
+                nc.sync.dma_start(
+                    out=w_raw[:, g, :, OUT:W_COLS],
+                    in_=Wgs[s][rows, :].rearrange("(p t) n -> p t n", t=PACK),
+                )
+
+        def quantise_weights():
+            nc.vector.tensor_scalar_mul(
+                out=w_raw[:, :, :, LAST_GATE_COL:W_COLS], in0=w_raw[:, :, :, LAST_GATE_COL:W_COLS],
+                scalar1=-1.0,
+            )
+            for g in range(PASSES):
+                regroup(nc, w_grouped[:, g, :, :], w_raw[:, g, :, :])
+            for g in range(PASSES):
+                nc.vector.quantize_mx(
+                    out=w_codes[:, g, :].bitcast(FP8X4),
+                    scales=w_scales[:, g, :],
+                    in_=w_grouped[:, g, :, :].rearrange("p n t -> p (n t)"),
+                )
+
+        x_blks = {}
+        partials = {}
+        rstds = {}
+        shifts = {}
+        x_norms = {}
+        planes_of = {}
+        grouped_of = {}
+        f_codes_of = {}
+        f_scales_of = {}
+        gate = {}
+
+        def load(b):
+            x_blks[b] = x_pool.tile([P, ROW_TILES, K_ALL], BF16, name="x_blk")
+            rows = slice(b * BLOCK, (b + 1) * BLOCK)
+            for s in range(NS):
+                k0 = PASSES_OF_STREAM[s][0] * K_PASS
+                k1 = (PASSES_OF_STREAM[s][-1] + 1) * K_PASS
+                nc.sync.dma_start(
+                    out=x_blks[b][:, :, k0:k1],
+                    in_=xs[s][rows, :].rearrange("(p t) k -> p t k", t=ROW_TILES),
+                )
+
+        def statistics(b, g):
+            if g == 0:
+                partials[b] = stat_pool.tile([P, ROW_TILES, PASSES, 6], F32, name="partial")
+            for t in range(ROW_TILES):
+                nc.vector.bn_stats(
+                    out=partials[b][:, t, g, :], in_=x_blks[b][:, t, g * K_PASS : (g + 1) * K_PASS]
+                )
+
+        def row_scalars(b, s):
+            g0 = PASSES_OF_STREAM[s][0]
+            g1 = PASSES_OF_STREAM[s][-1] + 1
+            mean_var = stat_pool.tile([P, ROW_TILES, 2], F32)
+            for t in range(ROW_TILES):
+                nc.vector.bn_aggr(
+                    out=mean_var[:, t, :],
+                    in_=partials[b][:, t, g0:g1, :].rearrange("p g v -> p (g v)"),
+                )
+            var_eps = stat_pool.tile([P, ROW_TILES], F32)
+            nc.vector.tensor_scalar_add(out=var_eps[:], in0=mean_var[:, :, 1], scalar1=EPS)
+            neg_mean = stat_pool.tile([P, ROW_TILES], F32)
+            nc.vector.tensor_scalar_mul(out=neg_mean[:], in0=mean_var[:, :, 0], scalar1=-1.0)
+            rstds[b, s] = stat_pool.tile([P, ROW_TILES], F32, name="rstd")
+            nc.gpsimd.tensor_tensor(out=rstds[b, s][:], in0=var_eps[:], in1=minus_half[:], op=ALU.pow)
+            shifts[b, s] = stat_pool.tile([P, ROW_TILES], F32, name="shift")
+            nc.gpsimd.tensor_mul(out=shifts[b, s][:], in0=neg_mean[:], in1=rstds[b, s][:])
+
+        def normalise(b, g):
+            s = STREAM_OF_PASS[g]
+            x_norms[b, g] = norm_pool.tile([P, ROW_TILES, PACK, P], F32, name="x_norm")
+            for t in range(ROW_TILES):
+                x_rows = x_blks[b][:, t, g * K_PASS : (g + 1) * K_PASS].rearrange(
+                    "p (h i j) -> p h j i", i=4, j=PACK
+                )
+                normed = x_norms[b, g][:, t, :, :].rearrange("p j (h i) -> p h j i", i=4)
+                rstd = rstds[b, s][:, t : t + 1]
+                shift = shifts[b, s][:, t : t + 1]
+                if t < VECTOR_ROW_TILES:
+                    nc.vector.tensor_scalar(
+                        out=normed, in0=x_rows, scalar1=rstd, scalar2=shift,
+                        op0=ALU.mult, op1=ALU.add,
+                    )
+                else:
+                    nc.scalar.activation(
+                        out=normed, in_=x_rows, func=ACT.Identity,
+                        scale=rstd, bias=shift,
+                    )
+
+        def transpose_and_scale(b, g):
+            planes_of[b, g] = plane_pool.tile([P, PACK, BLOCK], BF16, name="planes")
+            for j in range(PACK):
+                x_t = psum_xt.tile([P, BLOCK], F32, tag="xt")
+                for t in range(ROW_TILES):
+                    nc.tensor.transpose(
+                        x_t[:, t * P : (t + 1) * P], x_norms[b, g][:, t, j, :],
+                        ident_f32[:],
+                    )
+                nc.scalar.activation(
+                    out=planes_of[b, g][:, j, :], in_=x_t[:], func=ACT.Relu,
+                    scale=ln_param[:, 0, g, j : j + 1], bias=ln_param[:, 1, g, j : j + 1],
+                )
+
+        def regroup_features(b, g):
+            grouped_of[b, g] = f_pool.tile([P, BLOCK, PACK], BF16, name="grouped", align_bytes=64)
+            regroup(nc, grouped_of[b, g][:], planes_of[b, g][:])
+
+        def quantise_features(b, g):
+            if g == 0:
+                f_codes_of[b] = code_pool.tile([P, PASSES, BLOCK], U32, name="f_codes", align_bytes=64)
+                f_scales_of[b] = code_pool.tile([P, PASSES, BLOCK], U8, name="f_scales", align_bytes=64)
+            nc.vector.quantize_mx(
+                out=f_codes_of[b][:, g, :].bitcast(FP8X4),
+                scales=f_scales_of[b][:, g, :],
+                in_=grouped_of[b, g][:].rearrange("p r t -> p (r t)"),
+            )
+
+        def product(acc, b, passes, first_cols):
+            terms = [(g, c) for g in passes for c in first_cols]
+            for g, c in terms:
+                nc.tensor.matmul_mx(
+                    out=acc[:],
+                    lhsT=w_codes[:, g, c : c + P].bitcast(FP8X4), lhsT_scale=w_scales[:, g, c : c + P],
+                    rhs=f_codes_of[b][:, g, :].bitcast(FP8X4), rhs_scale=f_scales_of[b][:, g, :],
+                    start=((g, c) == terms[0]), stop=((g, c) == terms[-1]),
+                )
+
+        def sum_transposed(acc, terms):
+            for t in range(ROW_TILES):
+                for i in range(NS):
+                    nc.tensor.matmul(
+                        out=acc[:, t * P : (t + 1) * P], lhsT=terms[i][:, t * P : (t + 1) * P],
+                        rhs=ident_f32[:], is_transpose=True, start=(i == 0), stop=(i == NS - 1),
+                    )
+
+        def gate_tile(name):
+            gate[name] = gate_pool.tile([P, BLOCK], F32, name=name)
+            return gate[name]
+
+        def logit_difference(b, i):
+            gate["diff%d" % i] = psum_mx.tile([P, BLOCK], F32, name="diff%d" % i, tag="mx%d" % i)
+            product(gate["diff%d" % i], b, tuple(range(PASSES)), (OUT + i * OUT, LAST_GATE_COL))
+
+        def maximum_with_zero():
+            nc.scalar.activation(
+                out=gate_tile("top02")[:], in_=gate["diff0"][:], func=ACT.Relu,
+                bias=diff_bias[:, 0:1], scale=1.0,
+            )
+
+        def take_off_maximum():
+            nc.vector.scalar_tensor_tensor(
+                out=gate_tile("top")[:], in0=gate["diff1"][:], scalar=diff_bias[:, 1:2],
+                in1=gate["top02"][:], op0=ALU.add, op1=ALU.max,
+            )
+            for i in range(NS - 1):
+                nc.vector.scalar_tensor_tensor(
+                    out=gate_tile("below%d" % i)[:], in0=gate["diff%d" % i][:],
+                    scalar=diff_bias[:, i : i + 1], in1=gate["top"][:], op0=ALU.add, op1=ALU.subtract,
+                )
+
+        def exponentials(b):
+            for i in range(NS - 1):
+                nc.scalar.activation(
+                    out=gate_tile("expo%d" % i)[:], in_=gate["below%d" % i][:], func=ACT.Exp
+                )
+            nc.scalar.activation(
+                out=gate_tile("expo%d" % (NS - 1))[:], in_=gate["top"][:], func=ACT.Exp, scale=-1.0
+            )
+            for s in range(NS):
+                gate["y%d" % s] = psum_mx.tile([P, BLOCK], F32, name="y%d" % s, tag="mx%d" % s)
+                product(gate["y%d" % s], b, PASSES_OF_STREAM[s], (0,))
+
+        def weigh():
+            for s in range(NS):
+                nc.vector.scalar_tensor_tensor(
+                    out=gate_tile("weighted%d" % s)[:], in0=gate["y%d" % s][:],
+                    scalar=param[:, OUT_BIAS_ROW + s : OUT_BIAS_ROW + s + 1],
+                    in1=gate["expo%d" % s][:], op0=ALU.add, op1=ALU.mult,
+                )
+
+        def denominator():
+            gate["denom"] = psum_sn.tile([P, BLOCK], F32, name="denom")
+            sum_transposed(gate["denom"], [gate["expo%d" % i] for i in range(NS)])
+
+        def numerator():
+            gate["numer"] = psum_sn.tile([P, BLOCK], F32, name="numer")
+            sum_transposed(gate["numer"], [gate["weighted%d" % s] for s in range(NS)])
+            nc.scalar.activation(out=gate_tile("log_denom")[:], in_=gate["denom"][:], func=ACT.Ln)
+
+        def invert():
+            nc.scalar.activation(
+                out=gate_tile("inverse")[:], in_=gate["log_denom"][:], func=ACT.Exp, scale=-1.0
+            )
+
+        def finish(b):
+            merged = out_pool.tile([P, BLOCK], F32)
+            nc.vector.tensor_mul(out=merged[:], in0=gate["numer"][:], in1=gate["inverse"][:])
+            nc.sync.dma_start(
+                out=out[b * BLOCK : (b + 1) * BLOCK, :].rearrange("(p t) n -> p (t n)", t=ROW_TILES),
+                in_=merged[:],
+            )
+
+        def step(n):
+            def at(lag):
+                if 0 <= n - lag < N_BLOCKS * STEPS_PER_BLOCK:
+                    return divmod(n - lag, STEPS_PER_BLOCK)
+                return None
+
+            merging = at(MERGE_LAG)
+            if merging and merging[1] == 0:
+                logit_difference(merging[0], 0)
+            if merging and merging[1] == 1:
+                take_off_maximum()
+            if merging and merging[1] == 2:
+                weigh()
+                denominator()
+            if merging and merging[1] == 3:
+                invert()
+            if at(NORM_LAG):
+                normalise(*at(NORM_LAG))
+            if at(TRANSPOSE_LAG):
+                transpose_and_scale(*at(TRANSPOSE_LAG))
+            if at(QUANT_LAG):
+                quantise_features(*at(QUANT_LAG))
+            if at(0):
+                b, g = at(0)
+                statistics(b, g)
+                if g == PASSES_OF_STREAM[STREAM_OF_PASS[g]][-1]:
+                    row_scalars(b, STREAM_OF_PASS[g])
+                if g == 0 and b + 1 < N_BLOCKS:
+                    load(b + 1)
+            if at(REGROUP_LAG):
+                regroup_features(*at(REGROUP_LAG))
+            if merging and merging[1] == 0:
+                logit_difference(merging[0], 1)
+                maximum_with_zero()
+            if merging and merging[1] == 1:
+                exponentials(merging[0])
+            if merging and merging[1] == 2:
+                numerator()
+            if merging and merging[1] == 3:
+                finish(merging[0])
+
+        load(0)
+        load_small_vectors()
+        load_weights()
+        for n in range(REGROUP_LAG):
+            step(n)
+        quantise_weights()
+        for n in range(REGROUP_LAG, N_STEPS):
+            step(n)

@@ -27,7 +27,8 @@ PASSES_OF_STREAM = ((0,), (1,), (2, 3))
 W_COLS = OUT + NS * OUT
 LAST_GATE_COL = W_COLS - OUT
 EPS = 1e-5
-VECTOR_ROW_TILES = 1
+SCALAR_ROW_TILES = 1
+GROUPS = ((0, 1), (2, 3), (4, 5), (6,), (7,))
 
 OUT_BIAS_ROW = 0
 GATE_BIAS_ROW = OUT_BIAS_ROW + NS
@@ -38,12 +39,21 @@ LN_SLOT = 16
 FLOPS = 2 * ROWS * K_ALL * W_COLS
 
 STEPS_PER_BLOCK = PASSES
-NORM_LAG = 3
+LAST_PASS = tuple(passes[-1] for passes in PASSES_OF_STREAM)
+SCALARS_LAG = 1
+NORM_LAG = 4
 TRANSPOSE_LAG = NORM_LAG + 1
 REGROUP_LAG = TRANSPOSE_LAG + 1
 QUANT_LAG = REGROUP_LAG + 1
-MERGE_LAG = QUANT_LAG + STEPS_PER_BLOCK
-N_STEPS = N_BLOCKS * STEPS_PER_BLOCK + MERGE_LAG
+LOGIT_0_LAG = 1
+LOGIT_1_LAG = 2
+TOP_LAG = 3
+EXP_LAG = 4
+WEIGH_LAG = 5
+LOG_LAG = 5
+INVERT_LAG = 6
+FINISH_LAG = 7
+N_STEPS = N_BLOCKS * STEPS_PER_BLOCK + QUANT_LAG + FINISH_LAG
 
 
 def regroup(nc, grouped, planes):
@@ -71,17 +81,18 @@ def tile_vectormerge_pa_t_kernel(
 
     with ExitStack() as ctx:
         keep = ctx.enter_context(tc.tile_pool(name="keep", bufs=1))
-        x_pool = ctx.enter_context(tc.tile_pool(name="x_pool", bufs=3))
-        stat_pool = ctx.enter_context(tc.tile_pool(name="stat_pool", bufs=6))
+        x_pool = ctx.enter_context(tc.tile_pool(name="x_pool", bufs=4))
+        stat_pool = ctx.enter_context(tc.tile_pool(name="stat_pool", bufs=8))
         norm_pool = ctx.enter_context(tc.tile_pool(name="norm_pool", bufs=4))
         plane_pool = ctx.enter_context(tc.tile_pool(name="plane_pool", bufs=3))
         f_pool = ctx.enter_context(tc.tile_pool(name="f_pool", bufs=2))
         code_pool = ctx.enter_context(tc.tile_pool(name="code_pool", bufs=2))
         gate_pool = ctx.enter_context(tc.tile_pool(name="gate_pool", bufs=1))
+        term_pool = ctx.enter_context(tc.tile_pool(name="term_pool", bufs=2))
         out_pool = ctx.enter_context(tc.tile_pool(name="out_pool", bufs=2))
         psum_xt = ctx.enter_context(tc.psum_pool(name="psum_xt", bufs=3))
         psum_mx = ctx.enter_context(tc.psum_pool(name="psum_mx", bufs=1))
-        psum_sn = ctx.enter_context(tc.psum_pool(name="psum_sn", bufs=1))
+        psum_sn = ctx.enter_context(tc.psum_pool(name="psum_sn", bufs=2))
 
         ctx.enter_context(tc.manual_schedule())
 
@@ -160,12 +171,13 @@ def tile_vectormerge_pa_t_kernel(
                 )
 
         def quantise_weights():
-            nc.vector.tensor_scalar_mul(
-                out=w_raw[:, :, :, LAST_GATE_COL:W_COLS], in0=w_raw[:, :, :, LAST_GATE_COL:W_COLS],
-                scalar1=-1.0,
-            )
             for g in range(PASSES):
-                regroup(nc, w_grouped[:, g, :, :], w_raw[:, g, :, :])
+                for c0, c1, sign in ((0, LAST_GATE_COL, 1.0), (LAST_GATE_COL, W_COLS, -1.0)):
+                    nc.scalar.activation(
+                        out=w_grouped[:, g, c0:c1, :].rearrange("p (c i) t -> p c t i", i=4),
+                        in_=w_raw[:, g, :, c0:c1].rearrange("p t (c i) -> p c t i", i=4),
+                        func=ACT.Copy, scale=sign,
+                    )
             for g in range(PASSES):
                 nc.vector.quantize_mx(
                     out=w_codes[:, g, :].bitcast(FP8X4),
@@ -175,6 +187,7 @@ def tile_vectormerge_pa_t_kernel(
 
         x_blks = {}
         partials = {}
+        mean_vars = {}
         rstds = {}
         shifts = {}
         x_norms = {}
@@ -182,6 +195,7 @@ def tile_vectormerge_pa_t_kernel(
         grouped_of = {}
         f_codes_of = {}
         f_scales_of = {}
+        terms_of = {}
         gate = {}
 
         def load(b):
@@ -203,19 +217,21 @@ def tile_vectormerge_pa_t_kernel(
                     out=partials[b][:, t, g, :], in_=x_blks[b][:, t, g * K_PASS : (g + 1) * K_PASS]
                 )
 
-        def row_scalars(b, s):
+        def aggregate(b, s):
             g0 = PASSES_OF_STREAM[s][0]
             g1 = PASSES_OF_STREAM[s][-1] + 1
-            mean_var = stat_pool.tile([P, ROW_TILES, 2], F32)
+            mean_vars[b, s] = stat_pool.tile([P, ROW_TILES, 2], F32, name="mean_var")
             for t in range(ROW_TILES):
                 nc.vector.bn_aggr(
-                    out=mean_var[:, t, :],
+                    out=mean_vars[b, s][:, t, :],
                     in_=partials[b][:, t, g0:g1, :].rearrange("p g v -> p (g v)"),
                 )
+
+        def row_scalars(b, s):
             var_eps = stat_pool.tile([P, ROW_TILES], F32)
-            nc.vector.tensor_scalar_add(out=var_eps[:], in0=mean_var[:, :, 1], scalar1=EPS)
+            nc.vector.tensor_scalar_add(out=var_eps[:], in0=mean_vars[b, s][:, :, 1], scalar1=EPS)
             neg_mean = stat_pool.tile([P, ROW_TILES], F32)
-            nc.vector.tensor_scalar_mul(out=neg_mean[:], in0=mean_var[:, :, 0], scalar1=-1.0)
+            nc.vector.tensor_scalar_mul(out=neg_mean[:], in0=mean_vars[b, s][:, :, 0], scalar1=-1.0)
             rstds[b, s] = stat_pool.tile([P, ROW_TILES], F32, name="rstd")
             nc.gpsimd.tensor_tensor(out=rstds[b, s][:], in0=var_eps[:], in1=minus_half[:], op=ALU.pow)
             shifts[b, s] = stat_pool.tile([P, ROW_TILES], F32, name="shift")
@@ -231,15 +247,14 @@ def tile_vectormerge_pa_t_kernel(
                 normed = x_norms[b, g][:, t, :, :].rearrange("p j (h i) -> p h j i", i=4)
                 rstd = rstds[b, s][:, t : t + 1]
                 shift = shifts[b, s][:, t : t + 1]
-                if t < VECTOR_ROW_TILES:
-                    nc.vector.tensor_scalar(
-                        out=normed, in0=x_rows, scalar1=rstd, scalar2=shift,
-                        op0=ALU.mult, op1=ALU.add,
+                if t < SCALAR_ROW_TILES:
+                    nc.scalar.activation(
+                        out=normed, in_=x_rows, func=ACT.Identity, scale=rstd, bias=shift,
                     )
                 else:
-                    nc.scalar.activation(
-                        out=normed, in_=x_rows, func=ACT.Identity,
-                        scale=rstd, bias=shift,
+                    nc.gpsimd.tensor_scalar(
+                        out=normed, in0=x_rows, scalar1=rstd, scalar2=shift,
+                        op0=ALU.mult, op1=ALU.add,
                     )
 
         def transpose_and_scale(b, g):
@@ -292,21 +307,27 @@ def tile_vectormerge_pa_t_kernel(
             gate[name] = gate_pool.tile([P, BLOCK], F32, name=name)
             return gate[name]
 
+        def term_tile(b, name):
+            terms_of[b, name] = term_pool.tile([P, BLOCK], F32, name=name)
+            return terms_of[b, name]
+
         def logit_difference(b, i):
             gate["diff%d" % i] = psum_mx.tile([P, BLOCK], F32, name="diff%d" % i, tag="mx%d" % i)
             product(gate["diff%d" % i], b, tuple(range(PASSES)), (OUT + i * OUT, LAST_GATE_COL))
 
-        def maximum_with_zero():
+        def maximum_with_zero(b):
             nc.scalar.activation(
                 out=gate_tile("top02")[:], in_=gate["diff0"][:], func=ACT.Relu,
                 bias=diff_bias[:, 0:1], scale=1.0,
             )
 
-        def take_off_maximum():
+        def largest(b):
             nc.vector.scalar_tensor_tensor(
                 out=gate_tile("top")[:], in0=gate["diff1"][:], scalar=diff_bias[:, 1:2],
                 in1=gate["top02"][:], op0=ALU.add, op1=ALU.max,
             )
+
+        def take_off_maximum(b):
             for i in range(NS - 1):
                 nc.vector.scalar_tensor_tensor(
                     out=gate_tile("below%d" % i)[:], in0=gate["diff%d" % i][:],
@@ -316,44 +337,50 @@ def tile_vectormerge_pa_t_kernel(
         def exponentials(b):
             for i in range(NS - 1):
                 nc.scalar.activation(
-                    out=gate_tile("expo%d" % i)[:], in_=gate["below%d" % i][:], func=ACT.Exp
+                    out=term_tile(b, "expo%d" % i)[:], in_=gate["below%d" % i][:], func=ACT.Exp
                 )
             nc.scalar.activation(
-                out=gate_tile("expo%d" % (NS - 1))[:], in_=gate["top"][:], func=ACT.Exp, scale=-1.0
+                out=term_tile(b, "expo%d" % (NS - 1))[:], in_=gate["top"][:], func=ACT.Exp, scale=-1.0
             )
+
+        def stream_products(b):
             for s in range(NS):
                 gate["y%d" % s] = psum_mx.tile([P, BLOCK], F32, name="y%d" % s, tag="mx%d" % s)
                 product(gate["y%d" % s], b, PASSES_OF_STREAM[s], (0,))
 
-        def weigh():
+        def weigh(b):
             for s in range(NS):
                 nc.vector.scalar_tensor_tensor(
-                    out=gate_tile("weighted%d" % s)[:], in0=gate["y%d" % s][:],
+                    out=term_tile(b, "weighted%d" % s)[:], in0=gate["y%d" % s][:],
                     scalar=param[:, OUT_BIAS_ROW + s : OUT_BIAS_ROW + s + 1],
-                    in1=gate["expo%d" % s][:], op0=ALU.add, op1=ALU.mult,
+                    in1=terms_of[b, "expo%d" % s][:], op0=ALU.add, op1=ALU.mult,
                 )
 
-        def denominator():
-            gate["denom"] = psum_sn.tile([P, BLOCK], F32, name="denom")
-            sum_transposed(gate["denom"], [gate["expo%d" % i] for i in range(NS)])
+        def log_denominator(b):
+            denom = psum_sn.tile([P, BLOCK], F32, name="denom", tag="sn")
+            sum_transposed(denom, [terms_of[b, "expo%d" % i] for i in range(NS)])
+            nc.scalar.activation(out=term_tile(b, "log_denom")[:], in_=denom[:], func=ACT.Ln)
 
-        def numerator():
-            gate["numer"] = psum_sn.tile([P, BLOCK], F32, name="numer")
-            sum_transposed(gate["numer"], [gate["weighted%d" % s] for s in range(NS)])
-            nc.scalar.activation(out=gate_tile("log_denom")[:], in_=gate["denom"][:], func=ACT.Ln)
-
-        def invert():
+        def invert(b):
             nc.scalar.activation(
-                out=gate_tile("inverse")[:], in_=gate["log_denom"][:], func=ACT.Exp, scale=-1.0
+                out=term_tile(b, "inverse")[:], in_=terms_of[b, "log_denom"][:], func=ACT.Exp, scale=-1.0
             )
+
+        def numerator(b):
+            terms_of[b, "numer"] = psum_sn.tile([P, BLOCK], F32, name="numer", tag="sn")
+            sum_transposed(terms_of[b, "numer"], [terms_of[b, "weighted%d" % s] for s in range(NS)])
 
         def finish(b):
             merged = out_pool.tile([P, BLOCK], F32)
-            nc.vector.tensor_mul(out=merged[:], in0=gate["numer"][:], in1=gate["inverse"][:])
+            nc.vector.tensor_mul(
+                out=merged[:], in0=terms_of[b, "numer"][:], in1=terms_of[b, "inverse"][:]
+            )
             nc.sync.dma_start(
                 out=out[b * BLOCK : (b + 1) * BLOCK, :].rearrange("(p t) n -> p (t n)", t=ROW_TILES),
                 in_=merged[:],
             )
+
+        group_of_last = {group[-1]: group for group in GROUPS}
 
         def step(n):
             def at(lag):
@@ -361,46 +388,54 @@ def tile_vectormerge_pa_t_kernel(
                     return divmod(n - lag, STEPS_PER_BLOCK)
                 return None
 
-            merging = at(MERGE_LAG)
-            if merging and merging[1] == 0:
-                logit_difference(merging[0], 0)
-            if merging and merging[1] == 1:
-                take_off_maximum()
-            if merging and merging[1] == 2:
-                weigh()
-                denominator()
-            if merging and merging[1] == 3:
-                invert()
+            def merged(lag):
+                b, g = divmod(n - lag - QUANT_LAG, STEPS_PER_BLOCK)
+                return b if g == STEPS_PER_BLOCK - 1 and 0 <= b < N_BLOCKS else None
+
+            def run(lag, piece):
+                if merged(lag) is not None:
+                    piece(merged(lag))
+
+            def run_group(lag, piece):
+                for b in group_of_last.get(merged(lag), ()):
+                    piece(b)
+
+            run(LOGIT_1_LAG, lambda b: logit_difference(b, 1))
+            run(EXP_LAG, stream_products)
+            run(WEIGH_LAG, weigh)
+            run(TOP_LAG, largest)
+            run_group(FINISH_LAG, finish)
+            run_group(INVERT_LAG, invert)
+            run_group(INVERT_LAG, numerator)
+            if at(SCALARS_LAG) and at(SCALARS_LAG)[1] in LAST_PASS:
+                b, g = at(SCALARS_LAG)
+                row_scalars(b, STREAM_OF_PASS[g])
             if at(NORM_LAG):
                 normalise(*at(NORM_LAG))
-            if at(TRANSPOSE_LAG):
-                transpose_and_scale(*at(TRANSPOSE_LAG))
             if at(QUANT_LAG):
                 quantise_features(*at(QUANT_LAG))
+            run(TOP_LAG, take_off_maximum)
+            run(EXP_LAG, exponentials)
+            run(LOGIT_1_LAG, maximum_with_zero)
+            if at(TRANSPOSE_LAG):
+                transpose_and_scale(*at(TRANSPOSE_LAG))
             if at(0):
                 b, g = at(0)
                 statistics(b, g)
-                if g == PASSES_OF_STREAM[STREAM_OF_PASS[g]][-1]:
-                    row_scalars(b, STREAM_OF_PASS[g])
+                if g in LAST_PASS:
+                    aggregate(b, STREAM_OF_PASS[g])
                 if g == 0 and b + 1 < N_BLOCKS:
                     load(b + 1)
             if at(REGROUP_LAG):
                 regroup_features(*at(REGROUP_LAG))
-            if merging and merging[1] == 0:
-                logit_difference(merging[0], 1)
-                maximum_with_zero()
-            if merging and merging[1] == 1:
-                exponentials(merging[0])
-            if merging and merging[1] == 2:
-                numerator()
-            if merging and merging[1] == 3:
-                finish(merging[0])
+            run(LOGIT_0_LAG, lambda b: logit_difference(b, 0))
+            run_group(LOG_LAG, log_denominator)
 
         load(0)
         load_small_vectors()
         load_weights()
-        for n in range(REGROUP_LAG):
+        for n in range(TRANSPOSE_LAG):
             step(n)
         quantise_weights()
-        for n in range(REGROUP_LAG, N_STEPS):
+        for n in range(TRANSPOSE_LAG, N_STEPS):
             step(n)

@@ -22,45 +22,43 @@ OUT = 128
 NS = 3
 K_ALL = 2048
 PASSES = K_ALL // K_PASS
+N_ITEMS = N_BLOCKS * PASSES
 STREAM_OF_PASS = (0, 1, 2, 2)
 PASSES_OF_STREAM = ((0,), (1,), (2, 3))
+LAST_PASS = tuple(passes[-1] for passes in PASSES_OF_STREAM)
 W_COLS = OUT + NS * OUT
 LAST_GATE_COL = W_COLS - OUT
 EPS = 1e-5
-SCALAR_ROW_TILES = 1
-GROUPS = ((0, 1), (2, 3), (4, 5), (6,), (7,))
+LN_SLOT = 16
 
 OUT_BIAS_ROW = 0
 GATE_BIAS_ROW = OUT_BIAS_ROW + NS
-PARAM_ROWS = GATE_BIAS_ROW + NS * NS
 
-LN_SLOT = 16
+GROUPS = ((0, 1), (2, 3), (4, 5), (6,), (7,))
 
 FLOPS = 2 * ROWS * K_ALL * W_COLS
 
-STEPS_PER_BLOCK = PASSES
-LAST_PASS = tuple(passes[-1] for passes in PASSES_OF_STREAM)
-SCALARS_LAG = 1
-NORM_LAG = 4
-TRANSPOSE_LAG = NORM_LAG + 1
-REGROUP_LAG = TRANSPOSE_LAG + 1
-QUANT_LAG = REGROUP_LAG + 1
-LOGIT_0_LAG = 1
-LOGIT_1_LAG = 2
-TOP_LAG = 3
-EXP_LAG = 4
-WEIGH_LAG = 5
-LOG_LAG = 5
-INVERT_LAG = 6
-FINISH_LAG = 7
-N_STEPS = N_BLOCKS * STEPS_PER_BLOCK + QUANT_LAG + FINISH_LAG
+STATS_LEAD = 4
+RSTD_LEAD = 3
+SHIFT_LEAD = 2
+NORM_LEAD = 1
+REGROUP_LAG = 2
+QUANT_LAG = 3
+LOGIT_STEPS = {5: (0, 1), 6: (2,), 7: (3,)}
+TOP_STEP = 7
+BELOW_STEP = 8
+EXP_STEP = 8
+WEIGH_STEP = 9
+LOG_STEP = 10
+INVERT_STEP = 11
+FINISH_STEP = 11
+LATE_ITEM = N_ITEMS - STATS_LEAD
 
 
-def regroup(nc, grouped, planes):
-    nc.vector.tensor_copy(
-        out=grouped.rearrange("p (c i) t -> p c t i", i=4),
-        in_=planes.rearrange("p t (c i) -> p c t i", i=4),
-    )
+def norm_engine(i, t):
+    if i >= LATE_ITEM:
+        return ("gpsimd", "scalar", "vector", "vector")[t]
+    return ("gpsimd", "scalar", "scalar", "scalar")[t]
 
 
 def tile_vectormerge_pa_t_kernel(
@@ -81,18 +79,17 @@ def tile_vectormerge_pa_t_kernel(
 
     with ExitStack() as ctx:
         keep = ctx.enter_context(tc.tile_pool(name="keep", bufs=1))
-        x_pool = ctx.enter_context(tc.tile_pool(name="x_pool", bufs=4))
+        x_pool = ctx.enter_context(tc.tile_pool(name="x_pool", bufs=3))
         stat_pool = ctx.enter_context(tc.tile_pool(name="stat_pool", bufs=8))
-        norm_pool = ctx.enter_context(tc.tile_pool(name="norm_pool", bufs=4))
-        plane_pool = ctx.enter_context(tc.tile_pool(name="plane_pool", bufs=3))
-        f_pool = ctx.enter_context(tc.tile_pool(name="f_pool", bufs=2))
+        norm_pool = ctx.enter_context(tc.tile_pool(name="norm_pool", bufs=3))
+        plane_pool = ctx.enter_context(tc.tile_pool(name="plane_pool", bufs=4))
+        f_pool = ctx.enter_context(tc.tile_pool(name="f_pool", bufs=3))
         code_pool = ctx.enter_context(tc.tile_pool(name="code_pool", bufs=2))
         gate_pool = ctx.enter_context(tc.tile_pool(name="gate_pool", bufs=1))
         term_pool = ctx.enter_context(tc.tile_pool(name="term_pool", bufs=2))
         out_pool = ctx.enter_context(tc.tile_pool(name="out_pool", bufs=2))
         psum_xt = ctx.enter_context(tc.psum_pool(name="psum_xt", bufs=3))
         psum_mx = ctx.enter_context(tc.psum_pool(name="psum_mx", bufs=1))
-        psum_sn = ctx.enter_context(tc.psum_pool(name="psum_sn", bufs=2))
 
         ctx.enter_context(tc.manual_schedule())
 
@@ -114,14 +111,24 @@ def tile_vectormerge_pa_t_kernel(
         w_codes = keep.tile([P, PASSES, W_COLS], U32, align_bytes=64)
         w_scales = keep.tile([P, PASSES, W_COLS], U8, align_bytes=64)
 
-        def load_small_vectors():
+        def load_ln_vectors():
             for s in range(NS):
                 count = len(PASSES_OF_STREAM[s]) * PACK
-                for i, vec in enumerate((ln_ws[s], ln_bs[s])):
+                for j, vec in enumerate((ln_ws[s], ln_bs[s])):
                     nc.sync.dma_start(
-                        out=ln_raw[:, i, s, 0:count].rearrange("p (g j) -> p g j", j=PACK),
-                        in_=vec.rearrange("(g p j) -> p g j", p=P, j=PACK),
+                        out=ln_raw[:, j, s, 0:count].rearrange("p (g t) -> p g t", t=PACK),
+                        in_=vec.rearrange("(g p t) -> p g t", p=P, t=PACK),
                     )
+            for s in range(NS):
+                g0 = PASSES_OF_STREAM[s][0]
+                g1 = PASSES_OF_STREAM[s][-1] + 1
+                nc.scalar.copy(
+                    out=ln_param[:, :, g0:g1, :].rearrange("p j g t -> p j (g t)"),
+                    in_=ln_raw[:, :, s, 0 : (g1 - g0) * PACK],
+                )
+
+        def load_biases():
+            for s in range(NS):
                 nc.sync.dma_start(
                     out=param_rows[OUT_BIAS_ROW + s : OUT_BIAS_ROW + s + 1, :],
                     in_=bs[s].rearrange("(c p) -> c p", p=P),
@@ -130,16 +137,11 @@ def tile_vectormerge_pa_t_kernel(
                     out=param_rows[GATE_BIAS_ROW + NS * s : GATE_BIAS_ROW + NS * (s + 1), :],
                     in_=bgs[s].rearrange("(c p) -> c p", p=P),
                 )
+
+        def prepare_biases():
             param_ps = psum_xt.tile([P, P], BF16, tag="xt")
             nc.tensor.transpose(param_ps[:], param_rows[:], ident_bf16[:])
             nc.scalar.copy(out=param[:], in_=param_ps[:])
-            for s in range(NS):
-                g0 = PASSES_OF_STREAM[s][0]
-                g1 = PASSES_OF_STREAM[s][-1] + 1
-                nc.scalar.copy(
-                    out=ln_param[:, :, g0:g1, :].rearrange("p i g j -> p i (g j)"),
-                    in_=ln_raw[:, :, s, 0 : (g1 - g0) * PACK],
-                )
             nc.gpsimd.tensor_add(
                 out=gate_bias[:],
                 in0=param[:, GATE_BIAS_ROW : GATE_BIAS_ROW + NS],
@@ -156,39 +158,39 @@ def tile_vectormerge_pa_t_kernel(
                     in1=gate_bias[:, NS - 1 : NS],
                 )
 
-        def load_weights():
-            for g in range(PASSES):
-                s = STREAM_OF_PASS[g]
-                r0 = (g - PASSES_OF_STREAM[s][0]) * K_PASS
-                rows = slice(r0, r0 + K_PASS)
-                nc.sync.dma_start(
-                    out=w_raw[:, g, :, 0:OUT],
-                    in_=Ws[s][rows, :].rearrange("(p t) n -> p t n", t=PACK),
-                )
-                nc.sync.dma_start(
-                    out=w_raw[:, g, :, OUT:W_COLS],
-                    in_=Wgs[s][rows, :].rearrange("(p t) n -> p t n", t=PACK),
+        def load_weights(g):
+            s = STREAM_OF_PASS[g]
+            r0 = (g - PASSES_OF_STREAM[s][0]) * K_PASS
+            rows = slice(r0, r0 + K_PASS)
+            nc.sync.dma_start(
+                out=w_raw[:, g, :, 0:OUT],
+                in_=Ws[s][rows, :].rearrange("(p t) n -> p t n", t=PACK),
+            )
+            nc.sync.dma_start(
+                out=w_raw[:, g, :, OUT:W_COLS],
+                in_=Wgs[s][rows, :].rearrange("(p t) n -> p t n", t=PACK),
+            )
+
+        def regroup_weights(g):
+            for c0, c1, sign in ((0, LAST_GATE_COL, 1.0), (LAST_GATE_COL, W_COLS, -1.0)):
+                nc.scalar.activation(
+                    out=w_grouped[:, g, c0:c1, :].rearrange("p (c i) t -> p c t i", i=4),
+                    in_=w_raw[:, g, :, c0:c1].rearrange("p t (c i) -> p c t i", i=4),
+                    func=ACT.Copy, scale=sign,
                 )
 
-        def quantise_weights():
-            for g in range(PASSES):
-                for c0, c1, sign in ((0, LAST_GATE_COL, 1.0), (LAST_GATE_COL, W_COLS, -1.0)):
-                    nc.scalar.activation(
-                        out=w_grouped[:, g, c0:c1, :].rearrange("p (c i) t -> p c t i", i=4),
-                        in_=w_raw[:, g, :, c0:c1].rearrange("p t (c i) -> p c t i", i=4),
-                        func=ACT.Copy, scale=sign,
-                    )
-            for g in range(PASSES):
-                nc.vector.quantize_mx(
-                    out=w_codes[:, g, :].bitcast(FP8X4),
-                    scales=w_scales[:, g, :],
-                    in_=w_grouped[:, g, :, :].rearrange("p n t -> p (n t)"),
-                )
+        def quantise_weights(g):
+            nc.vector.quantize_mx(
+                out=w_codes[:, g, :].bitcast(FP8X4),
+                scales=w_scales[:, g, :],
+                in_=w_grouped[:, g, :, :].rearrange("p n t -> p (n t)"),
+            )
 
         x_blks = {}
         partials = {}
         mean_vars = {}
         rstds = {}
+        var_epses = {}
         shifts = {}
         x_norms = {}
         planes_of = {}
@@ -216,84 +218,97 @@ def tile_vectormerge_pa_t_kernel(
                 nc.vector.bn_stats(
                     out=partials[b][:, t, g, :], in_=x_blks[b][:, t, g * K_PASS : (g + 1) * K_PASS]
                 )
+            if g in LAST_PASS:
+                s = STREAM_OF_PASS[g]
+                g0 = PASSES_OF_STREAM[s][0]
+                mean_vars[b, s] = stat_pool.tile([P, ROW_TILES, 2], F32, name="mean_var")
+                for t in range(ROW_TILES):
+                    nc.vector.bn_aggr(
+                        out=mean_vars[b, s][:, t, :],
+                        in_=partials[b][:, t, g0 : g + 1, :].rearrange("p g v -> p (g v)"),
+                    )
 
-        def aggregate(b, s):
-            g0 = PASSES_OF_STREAM[s][0]
-            g1 = PASSES_OF_STREAM[s][-1] + 1
-            mean_vars[b, s] = stat_pool.tile([P, ROW_TILES, 2], F32, name="mean_var")
-            for t in range(ROW_TILES):
-                nc.vector.bn_aggr(
-                    out=mean_vars[b, s][:, t, :],
-                    in_=partials[b][:, t, g0:g1, :].rearrange("p g v -> p (g v)"),
+                var_epses[b, s] = stat_pool.tile([P, ROW_TILES], F32, name="var_eps")
+                nc.vector.tensor_scalar_add(
+                    out=var_epses[b, s][:], in0=mean_vars[b, s][:, :, 1], scalar1=EPS
                 )
 
-        def row_scalars(b, s):
-            var_eps = stat_pool.tile([P, ROW_TILES], F32)
-            nc.vector.tensor_scalar_add(out=var_eps[:], in0=mean_vars[b, s][:, :, 1], scalar1=EPS)
-            neg_mean = stat_pool.tile([P, ROW_TILES], F32)
-            nc.vector.tensor_scalar_mul(out=neg_mean[:], in0=mean_vars[b, s][:, :, 0], scalar1=-1.0)
+        def inverse_deviation(b, s):
             rstds[b, s] = stat_pool.tile([P, ROW_TILES], F32, name="rstd")
-            nc.gpsimd.tensor_tensor(out=rstds[b, s][:], in0=var_eps[:], in1=minus_half[:], op=ALU.pow)
-            shifts[b, s] = stat_pool.tile([P, ROW_TILES], F32, name="shift")
-            nc.gpsimd.tensor_mul(out=shifts[b, s][:], in0=neg_mean[:], in1=rstds[b, s][:])
+            nc.gpsimd.tensor_tensor(
+                out=rstds[b, s][:], in0=var_epses[b, s][:], in1=minus_half[:], op=ALU.pow
+            )
 
-        def normalise(b, g):
+        def mean_shift(b, s):
+            shifts[b, s] = stat_pool.tile([P, ROW_TILES], F32, name="shift")
+            nc.vector.scalar_tensor_tensor(
+                out=shifts[b, s][:], in0=mean_vars[b, s][:, :, 0], scalar=-1.0, in1=rstds[b, s][:],
+                op0=ALU.mult, op1=ALU.mult,
+            )
+
+        def normalise(i):
+            b, g = divmod(i, PASSES)
             s = STREAM_OF_PASS[g]
-            x_norms[b, g] = norm_pool.tile([P, ROW_TILES, PACK, P], F32, name="x_norm")
+            x_norms[i] = norm_pool.tile([P, ROW_TILES, PACK, P], F32, name="x_norm")
             for t in range(ROW_TILES):
                 x_rows = x_blks[b][:, t, g * K_PASS : (g + 1) * K_PASS].rearrange(
                     "p (h i j) -> p h j i", i=4, j=PACK
                 )
-                normed = x_norms[b, g][:, t, :, :].rearrange("p j (h i) -> p h j i", i=4)
-                rstd = rstds[b, s][:, t : t + 1]
-                shift = shifts[b, s][:, t : t + 1]
-                if t < SCALAR_ROW_TILES:
+                normed = x_norms[i][:, t, :, :].rearrange("p j (h i) -> p h j i", i=4)
+                scale = rstds[b, s][:, t : t + 1]
+                bias = shifts[b, s][:, t : t + 1]
+                if norm_engine(i, t) == "scalar":
                     nc.scalar.activation(
-                        out=normed, in_=x_rows, func=ACT.Identity, scale=rstd, bias=shift,
+                        out=normed, in_=x_rows, func=ACT.Identity, scale=scale, bias=bias
+                    )
+                elif norm_engine(i, t) == "vector":
+                    nc.vector.tensor_scalar(
+                        out=normed, in0=x_rows, scalar1=scale, scalar2=bias, op0=ALU.mult, op1=ALU.add
                     )
                 else:
                     nc.gpsimd.tensor_scalar(
-                        out=normed, in0=x_rows, scalar1=rstd, scalar2=shift,
-                        op0=ALU.mult, op1=ALU.add,
+                        out=normed, in0=x_rows, scalar1=scale, scalar2=bias, op0=ALU.mult, op1=ALU.add
                     )
 
-        def transpose_and_scale(b, g):
-            planes_of[b, g] = plane_pool.tile([P, PACK, BLOCK], BF16, name="planes")
+        def transpose_and_scale(i):
+            g = i % PASSES
+            planes_of[i] = plane_pool.tile([P, PACK, BLOCK], BF16, name="planes")
             for j in range(PACK):
                 x_t = psum_xt.tile([P, BLOCK], F32, tag="xt")
                 for t in range(ROW_TILES):
                     nc.tensor.transpose(
-                        x_t[:, t * P : (t + 1) * P], x_norms[b, g][:, t, j, :],
-                        ident_f32[:],
+                        x_t[:, t * P : (t + 1) * P], x_norms[i][:, t, j, :], ident_f32[:]
                     )
                 nc.scalar.activation(
-                    out=planes_of[b, g][:, j, :], in_=x_t[:], func=ACT.Relu,
+                    out=planes_of[i][:, j, :], in_=x_t[:], func=ACT.Relu,
                     scale=ln_param[:, 0, g, j : j + 1], bias=ln_param[:, 1, g, j : j + 1],
                 )
 
-        def regroup_features(b, g):
-            grouped_of[b, g] = f_pool.tile([P, BLOCK, PACK], BF16, name="grouped", align_bytes=64)
-            regroup(nc, grouped_of[b, g][:], planes_of[b, g][:])
+        def regroup_features(i):
+            grouped_of[i] = f_pool.tile([P, BLOCK, PACK], BF16, name="grouped", align_bytes=64)
+            nc.vector.tensor_copy(
+                out=grouped_of[i][:].rearrange("p (c i) t -> p c t i", i=4),
+                in_=planes_of[i][:].rearrange("p t (c i) -> p c t i", i=4),
+            )
 
-        def quantise_features(b, g):
+        def quantise_features(i):
+            b, g = divmod(i, PASSES)
             if g == 0:
                 f_codes_of[b] = code_pool.tile([P, PASSES, BLOCK], U32, name="f_codes", align_bytes=64)
                 f_scales_of[b] = code_pool.tile([P, PASSES, BLOCK], U8, name="f_scales", align_bytes=64)
             nc.vector.quantize_mx(
                 out=f_codes_of[b][:, g, :].bitcast(FP8X4),
                 scales=f_scales_of[b][:, g, :],
-                in_=grouped_of[b, g][:].rearrange("p r t -> p (r t)"),
+                in_=grouped_of[i][:].rearrange("p r t -> p (r t)"),
             )
 
-        def product(acc, b, passes, first_cols):
-            terms = [(g, c) for g in passes for c in first_cols]
-            for g, c in terms:
-                nc.tensor.matmul_mx(
-                    out=acc[:],
-                    lhsT=w_codes[:, g, c : c + P].bitcast(FP8X4), lhsT_scale=w_scales[:, g, c : c + P],
-                    rhs=f_codes_of[b][:, g, :].bitcast(FP8X4), rhs_scale=f_scales_of[b][:, g, :],
-                    start=((g, c) == terms[0]), stop=((g, c) == terms[-1]),
-                )
+        def product(acc, b, g, c, start, stop):
+            nc.tensor.matmul_mx(
+                out=acc[:],
+                lhsT=w_codes[:, g, c : c + P].bitcast(FP8X4), lhsT_scale=w_scales[:, g, c : c + P],
+                rhs=f_codes_of[b][:, g, :].bitcast(FP8X4), rhs_scale=f_scales_of[b][:, g, :],
+                start=start, stop=stop,
+            )
 
         def sum_transposed(acc, terms):
             for t in range(ROW_TILES):
@@ -311,9 +326,13 @@ def tile_vectormerge_pa_t_kernel(
             terms_of[b, name] = term_pool.tile([P, BLOCK], F32, name=name)
             return terms_of[b, name]
 
-        def logit_difference(b, i):
-            gate["diff%d" % i] = psum_mx.tile([P, BLOCK], F32, name="diff%d" % i, tag="mx%d" % i)
-            product(gate["diff%d" % i], b, tuple(range(PASSES)), (OUT + i * OUT, LAST_GATE_COL))
+        def logit_differences(b, passes):
+            for i in range(NS - 1):
+                if 0 in passes:
+                    gate["diff%d" % i] = psum_mx.tile([P, BLOCK], F32, name="diff%d" % i)
+                for g in passes:
+                    product(gate["diff%d" % i], b, g, OUT + i * OUT, g == 0, False)
+                    product(gate["diff%d" % i], b, g, LAST_GATE_COL, False, g == PASSES - 1)
 
         def maximum_with_zero(b):
             nc.scalar.activation(
@@ -321,7 +340,7 @@ def tile_vectormerge_pa_t_kernel(
                 bias=diff_bias[:, 0:1], scale=1.0,
             )
 
-        def largest(b):
+        def maximum(b):
             nc.vector.scalar_tensor_tensor(
                 out=gate_tile("top")[:], in0=gate["diff1"][:], scalar=diff_bias[:, 1:2],
                 in1=gate["top02"][:], op0=ALU.add, op1=ALU.max,
@@ -345,8 +364,10 @@ def tile_vectormerge_pa_t_kernel(
 
         def stream_products(b):
             for s in range(NS):
-                gate["y%d" % s] = psum_mx.tile([P, BLOCK], F32, name="y%d" % s, tag="mx%d" % s)
-                product(gate["y%d" % s], b, PASSES_OF_STREAM[s], (0,))
+                gate["y%d" % s] = psum_mx.tile([P, BLOCK], F32, name="y%d" % s, tag="y%d" % s)
+                passes = PASSES_OF_STREAM[s]
+                for g in passes:
+                    product(gate["y%d" % s], b, g, 0, g == passes[0], g == passes[-1])
 
         def weigh(b):
             for s in range(NS):
@@ -356,18 +377,22 @@ def tile_vectormerge_pa_t_kernel(
                     in1=terms_of[b, "expo%d" % s][:], op0=ALU.add, op1=ALU.mult,
                 )
 
+        def denominator(b, place):
+            terms_of[b, "denom"] = psum_mx.tile([P, BLOCK], F32, name="denom", tag="y%d" % place)
+            sum_transposed(terms_of[b, "denom"], [terms_of[b, "expo%d" % i] for i in range(NS)])
+
         def log_denominator(b):
-            denom = psum_sn.tile([P, BLOCK], F32, name="denom", tag="sn")
-            sum_transposed(denom, [terms_of[b, "expo%d" % i] for i in range(NS)])
-            nc.scalar.activation(out=term_tile(b, "log_denom")[:], in_=denom[:], func=ACT.Ln)
+            nc.scalar.activation(
+                out=term_tile(b, "log_denom")[:], in_=terms_of[b, "denom"][:], func=ACT.Ln
+            )
 
         def invert(b):
             nc.scalar.activation(
                 out=term_tile(b, "inverse")[:], in_=terms_of[b, "log_denom"][:], func=ACT.Exp, scale=-1.0
             )
 
-        def numerator(b):
-            terms_of[b, "numer"] = psum_sn.tile([P, BLOCK], F32, name="numer", tag="sn")
+        def numerator(b, place):
+            terms_of[b, "numer"] = psum_mx.tile([P, BLOCK], F32, name="numer", tag="y%d" % place)
             sum_transposed(terms_of[b, "numer"], [terms_of[b, "weighted%d" % s] for s in range(NS)])
 
         def finish(b):
@@ -382,60 +407,83 @@ def tile_vectormerge_pa_t_kernel(
 
         group_of_last = {group[-1]: group for group in GROUPS}
 
-        def step(n):
-            def at(lag):
-                if 0 <= n - lag < N_BLOCKS * STEPS_PER_BLOCK:
-                    return divmod(n - lag, STEPS_PER_BLOCK)
-                return None
+        def step(i):
+            def merging(offset):
+                b, g = divmod(i - offset, PASSES)
+                return (b,) if g == 0 and 0 <= b < N_BLOCKS else ()
 
-            def merged(lag):
-                b, g = divmod(n - lag - QUANT_LAG, STEPS_PER_BLOCK)
-                return b if g == STEPS_PER_BLOCK - 1 and 0 <= b < N_BLOCKS else None
+            def ending(offset):
+                return [b for last in merging(offset) for b in group_of_last.get(last, ())]
 
-            def run(lag, piece):
-                if merged(lag) is not None:
-                    piece(merged(lag))
+            def is_item(n):
+                return 0 <= n < N_ITEMS
 
-            def run_group(lag, piece):
-                for b in group_of_last.get(merged(lag), ()):
-                    piece(b)
+            def first_of_stream(n):
+                b, g = divmod(n, PASSES)
+                s = STREAM_OF_PASS[g]
+                return ((b, s),) if is_item(n) and g == PASSES_OF_STREAM[s][0] else ()
 
-            run(LOGIT_1_LAG, lambda b: logit_difference(b, 1))
-            run(EXP_LAG, stream_products)
-            run(WEIGH_LAG, weigh)
-            run(TOP_LAG, largest)
-            run_group(FINISH_LAG, finish)
-            run_group(INVERT_LAG, invert)
-            run_group(INVERT_LAG, numerator)
-            if at(SCALARS_LAG) and at(SCALARS_LAG)[1] in LAST_PASS:
-                b, g = at(SCALARS_LAG)
-                row_scalars(b, STREAM_OF_PASS[g])
-            if at(NORM_LAG):
-                normalise(*at(NORM_LAG))
-            if at(QUANT_LAG):
-                quantise_features(*at(QUANT_LAG))
-            run(TOP_LAG, take_off_maximum)
-            run(EXP_LAG, exponentials)
-            run(LOGIT_1_LAG, maximum_with_zero)
-            if at(TRANSPOSE_LAG):
-                transpose_and_scale(*at(TRANSPOSE_LAG))
-            if at(0):
-                b, g = at(0)
-                statistics(b, g)
-                if g in LAST_PASS:
-                    aggregate(b, STREAM_OF_PASS[g])
-                if g == 0 and b + 1 < N_BLOCKS:
-                    load(b + 1)
-            if at(REGROUP_LAG):
-                regroup_features(*at(REGROUP_LAG))
-            run(LOGIT_0_LAG, lambda b: logit_difference(b, 0))
-            run_group(LOG_LAG, log_denominator)
+            def last_of_stream(n):
+                b, g = divmod(n, PASSES)
+                return ((b, STREAM_OF_PASS[g]),) if is_item(n) and g in LAST_PASS else ()
+
+            for offset, passes in LOGIT_STEPS.items():
+                for b in merging(offset):
+                    logit_differences(b, passes)
+            for place, b in enumerate(ending(LOG_STEP)):
+                denominator(b, place)
+            for place, b in enumerate(ending(INVERT_STEP)):
+                numerator(b, (place + 2) % NS)
+            for b in merging(BELOW_STEP):
+                take_off_maximum(b)
+            for b in merging(WEIGH_STEP):
+                weigh(b)
+            for b in merging(EXP_STEP):
+                stream_products(b)
+            if is_item(i - QUANT_LAG):
+                quantise_features(i - QUANT_LAG)
+            if is_item(i - REGROUP_LAG):
+                regroup_features(i - REGROUP_LAG)
+            for b, s in last_of_stream(i + RSTD_LEAD):
+                inverse_deviation(b, s)
+            if is_item(i + NORM_LEAD):
+                normalise(i + NORM_LEAD)
+            for b, s in first_of_stream(i + SHIFT_LEAD):
+                mean_shift(b, s)
+            for b in merging(TOP_STEP):
+                maximum_with_zero(b)
+            for b in merging(EXP_STEP):
+                exponentials(b)
+            for b in ending(LOG_STEP):
+                log_denominator(b)
+            for b in ending(INVERT_STEP):
+                invert(b)
+            if is_item(i):
+                transpose_and_scale(i)
+            if is_item(i + STATS_LEAD):
+                statistics(*divmod(i + STATS_LEAD, PASSES))
+            for b in merging(TOP_STEP):
+                maximum(b)
+            for b in ending(FINISH_STEP):
+                finish(b)
+            for b in merging(0):
+                if 1 <= b and b + 2 < N_BLOCKS:
+                    load(b + 2)
 
         load(0)
-        load_small_vectors()
-        load_weights()
-        for n in range(TRANSPOSE_LAG):
-            step(n)
-        quantise_weights()
-        for n in range(TRANSPOSE_LAG, N_STEPS):
-            step(n)
+        load_ln_vectors()
+        for g in range(2):
+            load_weights(g)
+        load(1)
+        for g in range(2, PASSES):
+            load_weights(g)
+        load_biases()
+        load(2)
+        for i in range(-STATS_LEAD, N_ITEMS + FINISH_STEP - PASSES + 1):
+            step(i)
+            if i in range(1, 1 + PASSES):
+                regroup_weights(i - 1)
+            if i in range(2, 2 + PASSES):
+                quantise_weights(i - 2)
+            if i == 5:
+                prepare_biases()

@@ -25,7 +25,7 @@ PASSES = K_ALL // K_PASS
 N_ITEMS = N_BLOCKS * PASSES
 STREAM_OF_PASS = (0, 1, 2, 2)
 PASSES_OF_STREAM = ((0,), (1,), (2, 3))
-LAST_PASS = tuple(passes[-1] for passes in PASSES_OF_STREAM)
+STREAMS_OF_HALF = ((0, 1), (2,))
 W_COLS = OUT + NS * OUT
 LAST_GATE_COL = W_COLS - OUT
 EPS = 1e-5
@@ -40,7 +40,7 @@ FLOPS = 2 * ROWS * K_ALL * W_COLS
 
 STATS_LEAD = 4
 RSTD_LEAD = 3
-SHIFT_LEAD = 2
+SHIFT_LEAD = 3
 NORM_LEAD = 1
 REGROUP_LAG = 2
 QUANT_LAG = 3
@@ -58,7 +58,15 @@ LATE_ITEM = N_ITEMS - STATS_LEAD
 def norm_engine(i, t):
     if i >= LATE_ITEM:
         return ("gpsimd", "scalar", "vector", "vector")[t]
-    return ("gpsimd", "scalar", "scalar", "scalar")[t]
+    return ("gpsimd", "gpsimd", "gpsimd", "scalar")[t]
+
+
+def regroup_engine(i):
+    return "scalar" if i % 4 in (1, 3) and i < LATE_ITEM else "vector"
+
+
+def copy_engine(i, j):
+    return "vector" if i >= LATE_ITEM and j % 2 == 1 else "scalar"
 
 
 def tile_vectormerge_pa_t_kernel(
@@ -97,7 +105,7 @@ def tile_vectormerge_pa_t_kernel(
         make_identity(nc, ident_f32[:])
         ident_bf16 = keep.tile([P, P], BF16)
         make_identity(nc, ident_bf16[:])
-        minus_half = keep.tile([P, ROW_TILES], F32)
+        minus_half = keep.tile([P, 2, ROW_TILES], F32)
         nc.vector.memset(minus_half[:], -0.5)
         param_rows = keep.tile([P, P], BF16)
         nc.vector.memset(param_rows[:], 0.0)
@@ -218,45 +226,55 @@ def tile_vectormerge_pa_t_kernel(
                 nc.vector.bn_stats(
                     out=partials[b][:, t, g, :], in_=x_blks[b][:, t, g * K_PASS : (g + 1) * K_PASS]
                 )
-            if g in LAST_PASS:
-                s = STREAM_OF_PASS[g]
-                g0 = PASSES_OF_STREAM[s][0]
-                mean_vars[b, s] = stat_pool.tile([P, ROW_TILES, 2], F32, name="mean_var")
-                for t in range(ROW_TILES):
-                    nc.vector.bn_aggr(
-                        out=mean_vars[b, s][:, t, :],
-                        in_=partials[b][:, t, g0 : g + 1, :].rearrange("p g v -> p (g v)"),
-                    )
-
-                var_epses[b, s] = stat_pool.tile([P, ROW_TILES], F32, name="var_eps")
+            if g % 2 == 1:
+                h = g // 2
+                count = len(STREAMS_OF_HALF[h])
+                mean_vars[b, h] = stat_pool.tile([P, count, ROW_TILES, 2], F32, name="mean_var")
+                for k, s in enumerate(STREAMS_OF_HALF[h]):
+                    g0 = PASSES_OF_STREAM[s][0]
+                    g1 = PASSES_OF_STREAM[s][-1] + 1
+                    for t in range(ROW_TILES):
+                        nc.vector.bn_aggr(
+                            out=mean_vars[b, h][:, k, t, :],
+                            in_=partials[b][:, t, g0:g1, :].rearrange("p g v -> p (g v)"),
+                        )
+                var_epses[b, h] = stat_pool.tile([P, count, ROW_TILES], F32, name="var_eps")
                 nc.vector.tensor_scalar_add(
-                    out=var_epses[b, s][:], in0=mean_vars[b, s][:, :, 1], scalar1=EPS
+                    out=var_epses[b, h][:], in0=mean_vars[b, h][:, :, :, 1], scalar1=EPS
                 )
 
-        def inverse_deviation(b, s):
-            rstds[b, s] = stat_pool.tile([P, ROW_TILES], F32, name="rstd")
+        def inverse_deviation(b, h):
+            count = len(STREAMS_OF_HALF[h])
+            rstds[b, h] = stat_pool.tile([P, count, ROW_TILES], F32, name="rstd")
             nc.gpsimd.tensor_tensor(
-                out=rstds[b, s][:], in0=var_epses[b, s][:], in1=minus_half[:], op=ALU.pow
+                out=rstds[b, h][:], in0=var_epses[b, h][:], in1=minus_half[:, 0:count, :], op=ALU.pow
             )
 
-        def mean_shift(b, s):
-            shifts[b, s] = stat_pool.tile([P, ROW_TILES], F32, name="shift")
+        def mean_shift(b, h):
+            count = len(STREAMS_OF_HALF[h])
+            shifts[b, h] = stat_pool.tile([P, count, ROW_TILES], F32, name="shift")
             nc.vector.scalar_tensor_tensor(
-                out=shifts[b, s][:], in0=mean_vars[b, s][:, :, 0], scalar=-1.0, in1=rstds[b, s][:],
+                out=shifts[b, h][:], in0=mean_vars[b, h][:, :, :, 0], scalar=-1.0, in1=rstds[b, h][:],
                 op0=ALU.mult, op1=ALU.mult,
             )
 
         def normalise(i):
             b, g = divmod(i, PASSES)
-            s = STREAM_OF_PASS[g]
+            h = g // 2
+            k = STREAMS_OF_HALF[h].index(STREAM_OF_PASS[g])
+            late_shift = stat_pool.tile([P, ROW_TILES], F32)
+            nc.vector.scalar_tensor_tensor(
+                out=late_shift[:], in0=mean_vars[b, h][:, k, :, 0], scalar=-1.0, in1=rstds[b, h][:, k, :],
+                op0=ALU.mult, op1=ALU.mult,
+            )
             x_norms[i] = norm_pool.tile([P, ROW_TILES, PACK, P], F32, name="x_norm")
             for t in range(ROW_TILES):
                 x_rows = x_blks[b][:, t, g * K_PASS : (g + 1) * K_PASS].rearrange(
                     "p (h i j) -> p h j i", i=4, j=PACK
                 )
                 normed = x_norms[i][:, t, :, :].rearrange("p j (h i) -> p h j i", i=4)
-                scale = rstds[b, s][:, t : t + 1]
-                bias = shifts[b, s][:, t : t + 1]
+                scale = rstds[b, h][:, k, t : t + 1]
+                bias = shifts[b, h][:, k, t : t + 1]
                 if norm_engine(i, t) == "scalar":
                     nc.scalar.activation(
                         out=normed, in_=x_rows, func=ACT.Identity, scale=scale, bias=bias
@@ -267,7 +285,8 @@ def tile_vectormerge_pa_t_kernel(
                     )
                 else:
                     nc.gpsimd.tensor_scalar(
-                        out=normed, in0=x_rows, scalar1=scale, scalar2=bias, op0=ALU.mult, op1=ALU.add
+                        out=normed, in0=x_rows, scalar1=scale, scalar2=late_shift[:, t : t + 1],
+                        op0=ALU.mult, op1=ALU.add,
                     )
 
         def transpose_and_scale(i):
@@ -279,17 +298,26 @@ def tile_vectormerge_pa_t_kernel(
                     nc.tensor.transpose(
                         x_t[:, t * P : (t + 1) * P], x_norms[i][:, t, j, :], ident_f32[:]
                     )
-                nc.scalar.activation(
-                    out=planes_of[i][:, j, :], in_=x_t[:], func=ACT.Relu,
-                    scale=ln_param[:, 0, g, j : j + 1], bias=ln_param[:, 1, g, j : j + 1],
-                )
+                gain = ln_param[:, 0, g, j : j + 1]
+                offset = ln_param[:, 1, g, j : j + 1]
+                if copy_engine(i, j) == "scalar":
+                    nc.scalar.activation(
+                        out=planes_of[i][:, j, :], in_=x_t[:], func=ACT.Relu, scale=gain, bias=offset
+                    )
+                else:
+                    nc.vector.tensor_scalar(
+                        out=planes_of[i][:, j, :], in0=x_t[:], scalar1=gain, scalar2=offset,
+                        op0=ALU.mult, op1=ALU.add,
+                    )
 
         def regroup_features(i):
             grouped_of[i] = f_pool.tile([P, BLOCK, PACK], BF16, name="grouped", align_bytes=64)
-            nc.vector.tensor_copy(
-                out=grouped_of[i][:].rearrange("p (c i) t -> p c t i", i=4),
-                in_=planes_of[i][:].rearrange("p t (c i) -> p c t i", i=4),
-            )
+            grouped = grouped_of[i][:].rearrange("p (c i) t -> p c t i", i=4)
+            planes = planes_of[i][:].rearrange("p t (c i) -> p c t i", i=4)
+            if regroup_engine(i) == "scalar":
+                nc.scalar.activation(out=grouped, in_=planes, func=ACT.Relu)
+            else:
+                nc.vector.tensor_scalar_max(out=grouped, in0=planes, scalar1=0.0)
 
         def quantise_features(i):
             b, g = divmod(i, PASSES)
@@ -354,13 +382,13 @@ def tile_vectormerge_pa_t_kernel(
                 )
 
         def exponentials(b):
+            nc.scalar.activation(
+                out=term_tile(b, "expo%d" % (NS - 1))[:], in_=gate["top"][:], func=ACT.Exp, scale=-1.0
+            )
             for i in range(NS - 1):
                 nc.scalar.activation(
                     out=term_tile(b, "expo%d" % i)[:], in_=gate["below%d" % i][:], func=ACT.Exp
                 )
-            nc.scalar.activation(
-                out=term_tile(b, "expo%d" % (NS - 1))[:], in_=gate["top"][:], func=ACT.Exp, scale=-1.0
-            )
 
         def stream_products(b):
             for s in range(NS):
@@ -370,7 +398,7 @@ def tile_vectormerge_pa_t_kernel(
                     product(gate["y%d" % s], b, g, 0, g == passes[0], g == passes[-1])
 
         def weigh(b):
-            for s in range(NS):
+            for s in (NS - 1, *range(NS - 1)):
                 nc.vector.scalar_tensor_tensor(
                     out=term_tile(b, "weighted%d" % s)[:], in0=gate["y%d" % s][:],
                     scalar=param[:, OUT_BIAS_ROW + s : OUT_BIAS_ROW + s + 1],
@@ -418,14 +446,9 @@ def tile_vectormerge_pa_t_kernel(
             def is_item(n):
                 return 0 <= n < N_ITEMS
 
-            def first_of_stream(n):
+            def half_ends(n):
                 b, g = divmod(n, PASSES)
-                s = STREAM_OF_PASS[g]
-                return ((b, s),) if is_item(n) and g == PASSES_OF_STREAM[s][0] else ()
-
-            def last_of_stream(n):
-                b, g = divmod(n, PASSES)
-                return ((b, STREAM_OF_PASS[g]),) if is_item(n) and g in LAST_PASS else ()
+                return ((b, g // 2),) if is_item(n) and g % 2 == 1 else ()
 
             for offset, passes in LOGIT_STEPS.items():
                 for b in merging(offset):
@@ -433,7 +456,7 @@ def tile_vectormerge_pa_t_kernel(
             for place, b in enumerate(ending(LOG_STEP)):
                 denominator(b, place)
             for place, b in enumerate(ending(INVERT_STEP)):
-                numerator(b, (place + 2) % NS)
+                numerator(b, place)
             for b in merging(BELOW_STEP):
                 take_off_maximum(b)
             for b in merging(WEIGH_STEP):
@@ -444,12 +467,10 @@ def tile_vectormerge_pa_t_kernel(
                 quantise_features(i - QUANT_LAG)
             if is_item(i - REGROUP_LAG):
                 regroup_features(i - REGROUP_LAG)
-            for b, s in last_of_stream(i + RSTD_LEAD):
-                inverse_deviation(b, s)
+            for b, h in half_ends(i + RSTD_LEAD):
+                inverse_deviation(b, h)
             if is_item(i + NORM_LEAD):
                 normalise(i + NORM_LEAD)
-            for b, s in first_of_stream(i + SHIFT_LEAD):
-                mean_shift(b, s)
             for b in merging(TOP_STEP):
                 maximum_with_zero(b)
             for b in merging(EXP_STEP):
@@ -466,23 +487,28 @@ def tile_vectormerge_pa_t_kernel(
                 maximum(b)
             for b in ending(FINISH_STEP):
                 finish(b)
+            for b, h in half_ends(i + SHIFT_LEAD):
+                mean_shift(b, h)
             for b in merging(0):
                 if 1 <= b and b + 2 < N_BLOCKS:
                     load(b + 2)
 
         load(0)
         load_ln_vectors()
-        for g in range(2):
+        for g in range(PASSES):
             load_weights(g)
         load(1)
-        for g in range(2, PASSES):
-            load_weights(g)
         load_biases()
         load(2)
         for i in range(-STATS_LEAD, N_ITEMS + FINISH_STEP - PASSES + 1):
             step(i)
-            if i in range(1, 1 + PASSES):
-                regroup_weights(i - 1)
+            if i == -2:
+                regroup_weights(0)
+                regroup_weights(1)
+            if i == 1:
+                regroup_weights(2)
+            if i == 2:
+                regroup_weights(3)
             if i in range(2, 2 + PASSES):
                 quantise_weights(i - 2)
             if i == 5:

@@ -34,12 +34,12 @@ LN_SLOT = 16
 OUT_BIAS_ROW = 0
 GATE_BIAS_ROW = OUT_BIAS_ROW + NS
 
-GROUPS = ((0, 1), (2, 3), (4, 5), (6,), (7,))
+GROUPS = ((0, 1), (2, 3), (4, 5), (6, 7))
 
 FLOPS = 2 * ROWS * K_ALL * W_COLS
 
-STATS_LEAD = 4
-RSTD_LEAD = 3
+STATS_LEAD = 5
+RSTD_LEAD = 4
 SHIFT_LEAD = 3
 NORM_LEAD = 1
 REGROUP_LAG = 2
@@ -57,16 +57,16 @@ LATE_ITEM = N_ITEMS - STATS_LEAD
 
 def norm_engine(i, t):
     if i >= LATE_ITEM:
-        return ("gpsimd", "scalar", "vector", "vector")[t]
-    return ("gpsimd", "gpsimd", "gpsimd", "scalar")[t]
+        return ("gpsimd", "gpsimd", "scalar", "vector")[t]
+    return ("gpsimd", "gpsimd", "scalar" if i % 2 else "gpsimd", "scalar")[t]
 
 
 def regroup_engine(i):
-    return "scalar" if i % 4 in (1, 3) and i < LATE_ITEM else "vector"
+    return "scalar" if i % 4 == 3 and i < LATE_ITEM else "vector"
 
 
 def copy_engine(i, j):
-    return "vector" if i >= LATE_ITEM and j % 2 == 1 else "scalar"
+    return "vector" if False else "scalar"
 
 
 def tile_vectormerge_pa_t_kernel(
@@ -199,6 +199,7 @@ def tile_vectormerge_pa_t_kernel(
         mean_vars = {}
         rstds = {}
         var_epses = {}
+        late_shifts = {}
         shifts = {}
         x_norms = {}
         planes_of = {}
@@ -238,10 +239,13 @@ def tile_vectormerge_pa_t_kernel(
                             out=mean_vars[b, h][:, k, t, :],
                             in_=partials[b][:, t, g0:g1, :].rearrange("p g v -> p (g v)"),
                         )
-                var_epses[b, h] = stat_pool.tile([P, count, ROW_TILES], F32, name="var_eps")
-                nc.vector.tensor_scalar_add(
-                    out=var_epses[b, h][:], in0=mean_vars[b, h][:, :, :, 1], scalar1=EPS
-                )
+
+        def add_epsilon(b, h):
+            count = len(STREAMS_OF_HALF[h])
+            var_epses[b, h] = stat_pool.tile([P, count, ROW_TILES], F32, name="var_eps")
+            nc.vector.tensor_scalar_add(
+                out=var_epses[b, h][:], in0=mean_vars[b, h][:, :, :, 1], scalar1=EPS
+            )
 
         def inverse_deviation(b, h):
             count = len(STREAMS_OF_HALF[h])
@@ -250,31 +254,27 @@ def tile_vectormerge_pa_t_kernel(
                 out=rstds[b, h][:], in0=var_epses[b, h][:], in1=minus_half[:, 0:count, :], op=ALU.pow
             )
 
-        def mean_shift(b, h):
-            count = len(STREAMS_OF_HALF[h])
-            shifts[b, h] = stat_pool.tile([P, count, ROW_TILES], F32, name="shift")
-            nc.vector.scalar_tensor_tensor(
-                out=shifts[b, h][:], in0=mean_vars[b, h][:, :, :, 0], scalar=-1.0, in1=rstds[b, h][:],
-                op0=ALU.mult, op1=ALU.mult,
-            )
-
-        def normalise(i):
+        def normalise(i, engines):
             b, g = divmod(i, PASSES)
             h = g // 2
             k = STREAMS_OF_HALF[h].index(STREAM_OF_PASS[g])
-            late_shift = stat_pool.tile([P, ROW_TILES], F32)
-            nc.vector.scalar_tensor_tensor(
-                out=late_shift[:], in0=mean_vars[b, h][:, k, :, 0], scalar=-1.0, in1=rstds[b, h][:, k, :],
-                op0=ALU.mult, op1=ALU.mult,
-            )
-            x_norms[i] = norm_pool.tile([P, ROW_TILES, PACK, P], F32, name="x_norm")
+            if "gpsimd" in engines:
+                late_shifts[i] = stat_pool.tile([P, ROW_TILES], F32, name="late_shift")
+                nc.vector.scalar_tensor_tensor(
+                    out=late_shifts[i][:], in0=mean_vars[b, h][:, k, :, 0], scalar=-1.0,
+                    in1=rstds[b, h][:, k, :], op0=ALU.mult, op1=ALU.mult,
+                )
+                x_norms[i] = norm_pool.tile([P, ROW_TILES, PACK, P], F32, name="x_norm")
+            late_shift = late_shifts[i]
             for t in range(ROW_TILES):
+                if norm_engine(i, t) not in engines:
+                    continue
                 x_rows = x_blks[b][:, t, g * K_PASS : (g + 1) * K_PASS].rearrange(
                     "p (h i j) -> p h j i", i=4, j=PACK
                 )
                 normed = x_norms[i][:, t, :, :].rearrange("p j (h i) -> p h j i", i=4)
                 scale = rstds[b, h][:, k, t : t + 1]
-                bias = shifts[b, h][:, k, t : t + 1]
+                bias = late_shift[:, t : t + 1]
                 if norm_engine(i, t) == "scalar":
                     nc.scalar.activation(
                         out=normed, in_=x_rows, func=ACT.Identity, scale=scale, bias=bias
@@ -450,6 +450,8 @@ def tile_vectormerge_pa_t_kernel(
                 b, g = divmod(n, PASSES)
                 return ((b, g // 2),) if is_item(n) and g % 2 == 1 else ()
 
+            for b, h in half_ends(i + RSTD_LEAD):
+                add_epsilon(b, h)
             for offset, passes in LOGIT_STEPS.items():
                 for b in merging(offset):
                     logit_differences(b, passes)
@@ -467,10 +469,10 @@ def tile_vectormerge_pa_t_kernel(
                 quantise_features(i - QUANT_LAG)
             if is_item(i - REGROUP_LAG):
                 regroup_features(i - REGROUP_LAG)
+            if is_item(i + NORM_LEAD):
+                normalise(i + NORM_LEAD, ("gpsimd", "vector"))
             for b, h in half_ends(i + RSTD_LEAD):
                 inverse_deviation(b, h)
-            if is_item(i + NORM_LEAD):
-                normalise(i + NORM_LEAD)
             for b in merging(TOP_STEP):
                 maximum_with_zero(b)
             for b in merging(EXP_STEP):
@@ -481,14 +483,14 @@ def tile_vectormerge_pa_t_kernel(
                 invert(b)
             if is_item(i):
                 transpose_and_scale(i)
+            if is_item(i + NORM_LEAD):
+                normalise(i + NORM_LEAD, ("scalar",))
             if is_item(i + STATS_LEAD):
                 statistics(*divmod(i + STATS_LEAD, PASSES))
             for b in merging(TOP_STEP):
                 maximum(b)
             for b in ending(FINISH_STEP):
                 finish(b)
-            for b, h in half_ends(i + SHIFT_LEAD):
-                mean_shift(b, h)
             for b in merging(0):
                 if 1 <= b and b + 2 < N_BLOCKS:
                     load(b + 2)

@@ -45,24 +45,26 @@ NORM_LEAD = 1
 REGROUP_LAG = 2
 QUANT_LAG = 3
 LOGIT_STEPS = {5: (0, 1), 6: (2,), 7: (3,)}
+TAIL_GAIN = 2
+LAST_LOGIT_STEPS = {4: (0, 1, 2), 5: (3,)}
 TOP_STEP = 7
 BELOW_STEP = 8
 EXP_STEP = 8
 WEIGH_STEP = 9
 LOG_STEP = 10
 INVERT_STEP = 11
-FINISH_STEP = 11
+FINISH_STEP = 12
 LATE_ITEM = N_ITEMS - STATS_LEAD
 
 
 def norm_engine(i, t):
     if i >= LATE_ITEM:
         return ("gpsimd", "gpsimd", "scalar", "vector")[t]
-    return ("gpsimd", "gpsimd", "scalar" if i % 2 else "gpsimd", "scalar")[t]
+    return ("gpsimd", "gpsimd", "gpsimd", "scalar")[t]
 
 
 def regroup_engine(i):
-    return "scalar" if i % 4 == 3 and i < LATE_ITEM else "vector"
+    return "scalar" if i % 8 in (1, 3, 7) and i < LATE_ITEM else "vector"
 
 
 def copy_engine(i, j):
@@ -405,8 +407,8 @@ def tile_vectormerge_pa_t_kernel(
                     in1=terms_of[b, "expo%d" % s][:], op0=ALU.add, op1=ALU.mult,
                 )
 
-        def denominator(b, place):
-            terms_of[b, "denom"] = psum_mx.tile([P, BLOCK], F32, name="denom", tag="y%d" % place)
+        def denominator(b, pool, tag):
+            terms_of[b, "denom"] = pool.tile([P, BLOCK], F32, name="denom", tag=tag)
             sum_transposed(terms_of[b, "denom"], [terms_of[b, "expo%d" % i] for i in range(NS)])
 
         def log_denominator(b):
@@ -419,8 +421,8 @@ def tile_vectormerge_pa_t_kernel(
                 out=term_tile(b, "inverse")[:], in_=terms_of[b, "log_denom"][:], func=ACT.Exp, scale=-1.0
             )
 
-        def numerator(b, place):
-            terms_of[b, "numer"] = psum_mx.tile([P, BLOCK], F32, name="numer", tag="y%d" % place)
+        def numerator(b, pool, tag):
+            terms_of[b, "numer"] = pool.tile([P, BLOCK], F32, name="numer", tag=tag)
             sum_transposed(terms_of[b, "numer"], [terms_of[b, "weighted%d" % s] for s in range(NS)])
 
         def finish(b):
@@ -435,10 +437,23 @@ def tile_vectormerge_pa_t_kernel(
 
         group_of_last = {group[-1]: group for group in GROUPS}
 
+        def merge_step(b, offset):
+            return b * PASSES + offset - (TAIL_GAIN if b == N_BLOCKS - 1 else 0)
+
+        def weighed(i, offset):
+            return tuple(
+                b for b in range(N_BLOCKS) if merge_step(b, offset) + (1 if b == N_BLOCKS - 2 else 0) == i
+            )
+
+        def lag_of(k, lag):
+            return 1 if k >= N_ITEMS - PASSES else lag
+
+        def items_due(i, lag):
+            return [k for k in range(N_ITEMS) if k + lag_of(k, lag) == i]
+
         def step(i):
             def merging(offset):
-                b, g = divmod(i - offset, PASSES)
-                return (b,) if g == 0 and 0 <= b < N_BLOCKS else ()
+                return tuple(b for b in range(N_BLOCKS) if merge_step(b, offset) == i)
 
             def ending(offset):
                 return [b for last in merging(offset) for b in group_of_last.get(last, ())]
@@ -452,23 +467,41 @@ def tile_vectormerge_pa_t_kernel(
 
             for b, h in half_ends(i + RSTD_LEAD):
                 add_epsilon(b, h)
-            for offset, passes in LOGIT_STEPS.items():
-                for b in merging(offset):
-                    logit_differences(b, passes)
-            for place, b in enumerate(ending(LOG_STEP)):
-                denominator(b, place)
-            for place, b in enumerate(ending(INVERT_STEP)):
-                numerator(b, place)
             for b in merging(BELOW_STEP):
                 take_off_maximum(b)
+            for b in ending(FINISH_STEP):
+                finish(b)
+            for b in range(N_BLOCKS):
+                passes = (LAST_LOGIT_STEPS if b == N_BLOCKS - 1 else LOGIT_STEPS).get(i - b * PASSES, ())
+                logit_differences(b, passes)
+            for place, b in enumerate(ending(LOG_STEP)):
+                if b not in GROUPS[-1]:
+                    denominator(b, psum_mx, "y%d" % place)
+            for place, b in enumerate(ending(INVERT_STEP)):
+                if b not in GROUPS[-1]:
+                    numerator(b, psum_mx, "y%d" % place)
             for b in merging(WEIGH_STEP):
+                if b == N_BLOCKS - 2:
+                    denominator(b, psum_xt, "xt")
+            for b in weighed(i, LOG_STEP):
+                if b == N_BLOCKS - 2:
+                    numerator(b, psum_xt, "xt")
+            for b in merging(INVERT_STEP):
+                if b == N_BLOCKS - 1:
+                    numerator(b, psum_xt, "xt")
+            for b in weighed(i, WEIGH_STEP):
                 weigh(b)
-            for b in merging(EXP_STEP):
-                stream_products(b)
-            if is_item(i - QUANT_LAG):
-                quantise_features(i - QUANT_LAG)
-            if is_item(i - REGROUP_LAG):
-                regroup_features(i - REGROUP_LAG)
+            for b in weighed(i, EXP_STEP):
+                if b < N_BLOCKS - 1:
+                    stream_products(b)
+            for k in items_due(i, QUANT_LAG):
+                if k < N_ITEMS - PASSES:
+                    quantise_features(k)
+            for k in items_due(i, REGROUP_LAG):
+                regroup_features(k)
+            for k in items_due(i, QUANT_LAG):
+                if k >= N_ITEMS - PASSES:
+                    quantise_features(k)
             if is_item(i + NORM_LEAD):
                 normalise(i + NORM_LEAD, ("gpsimd", "vector"))
             for b, h in half_ends(i + RSTD_LEAD):
@@ -477,6 +510,9 @@ def tile_vectormerge_pa_t_kernel(
                 maximum_with_zero(b)
             for b in merging(EXP_STEP):
                 exponentials(b)
+                if b == N_BLOCKS - 1:
+                    denominator(b, psum_xt, "xt")
+                    stream_products(b)
             for b in ending(LOG_STEP):
                 log_denominator(b)
             for b in ending(INVERT_STEP):
@@ -489,11 +525,8 @@ def tile_vectormerge_pa_t_kernel(
                 statistics(*divmod(i + STATS_LEAD, PASSES))
             for b in merging(TOP_STEP):
                 maximum(b)
-            for b in ending(FINISH_STEP):
-                finish(b)
-            for b in merging(0):
-                if 1 <= b and b + 2 < N_BLOCKS:
-                    load(b + 2)
+            if i % PASSES == 0 and 1 <= i // PASSES < N_BLOCKS - 2:
+                load(i // PASSES + 2)
 
         load(0)
         load_ln_vectors()
@@ -502,7 +535,7 @@ def tile_vectormerge_pa_t_kernel(
         load(1)
         load_biases()
         load(2)
-        for i in range(-STATS_LEAD, N_ITEMS + FINISH_STEP - PASSES + 1):
+        for i in range(-STATS_LEAD, N_ITEMS - PASSES + FINISH_STEP - TAIL_GAIN + 1):
             step(i)
             if i == -2:
                 regroup_weights(0)

from contextlib import ExitStack

import concourse.mybir as mybir
from concourse.masks import make_identity

F32 = mybir.dt.float32
BF16 = mybir.dt.bfloat16
U32 = mybir.dt.uint32
U8 = mybir.dt.uint8
FP8X4 = mybir.dt.float8_e4m3fn_x4
ALU = mybir.AluOpType
ACT = mybir.ActivationFunctionType

P = 128
PACK = 4
K_PASS = P * PACK
ROWS = 4096
BLOCK = 512
ROW_TILES = BLOCK // P
N_BLOCKS = ROWS // BLOCK
OUT = 128
NS = 3
K_ALL = 2048
PASSES = K_ALL // K_PASS
N_ITEMS = N_BLOCKS * PASSES
STREAM_OF_PASS = (0, 1, 2, 2)
PASSES_OF_STREAM = ((0,), (1,), (2, 3))
STREAMS_OF_HALF = ((0, 1), (2,))
W_COLS = OUT + NS * OUT
LAST_GATE_COL = W_COLS - OUT
EPS = 1e-5
LN_SLOT = 16

OUT_BIAS_ROW = 0
GATE_BIAS_ROW = OUT_BIAS_ROW + NS

GROUPS = ((0, 1), (2, 3), (4, 5), (6, 7))

FLOPS = 2 * ROWS * K_ALL * W_COLS

STATS_LEAD = 5
RSTD_LEAD = 4
SHIFT_LEAD = 3
NORM_LEAD = 1
REGROUP_LAG = 2
QUANT_LAG = 3
LOGIT_STEPS = {5: (0, 1), 6: (2,), 7: (3,)}
TAIL_GAIN = 2
LAST_LOGIT_STEPS = {4: (0, 1, 2), 5: (3,)}
TOP_STEP = 7
BELOW_STEP = 8
EXP_STEP = 8
WEIGH_STEP = 9
LOG_STEP = 10
INVERT_STEP = 11
FINISH_STEP = 12
LATE_ITEM = N_ITEMS - STATS_LEAD


def norm_engine(i, t):
    if i >= LATE_ITEM:
        return ("gpsimd", "gpsimd", "scalar", "vector")[t]
    return ("gpsimd", "gpsimd", "gpsimd", "scalar")[t]


def regroup_engine(i):
    return "scalar" if i % 8 in (1, 3, 7) and i < LATE_ITEM else "vector"


def copy_engine(i, j):
    return "vector" if False else "scalar"


def tile_vectormerge_pa_t_kernel(
    tc,
    x_a, ln_w_a, ln_b_a, W_a, b_a, Wg_a, bg_a,
    x_b, ln_w_b, ln_b_b, W_b, b_b, Wg_b, bg_b,
    x_c, ln_w_c, ln_b_c, W_c, b_c, Wg_c, bg_c,
    out,
):
    nc = tc.nc
    xs = (x_a, x_b, x_c)
    ln_ws = (ln_w_a, ln_w_b, ln_w_c)
    ln_bs = (ln_b_a, ln_b_b, ln_b_c)
    Ws = (W_a, W_b, W_c)
    bs = (b_a, b_b, b_c)
    Wgs = (Wg_a, Wg_b, Wg_c)
    bgs = (bg_a, bg_b, bg_c)

    with ExitStack() as ctx:
        keep = ctx.enter_context(tc.tile_pool(name="keep", bufs=1))
        x_pool = ctx.enter_context(tc.tile_pool(name="x_pool", bufs=3))
        stat_pool = ctx.enter_context(tc.tile_pool(name="stat_pool", bufs=8))
        norm_pool = ctx.enter_context(tc.tile_pool(name="norm_pool", bufs=3))
        plane_pool = ctx.enter_context(tc.tile_pool(name="plane_pool", bufs=4))
        f_pool = ctx.enter_context(tc.tile_pool(name="f_pool", bufs=3))
        code_pool = ctx.enter_context(tc.tile_pool(name="code_pool", bufs=2))
        gate_pool = ctx.enter_context(tc.tile_pool(name="gate_pool", bufs=1))
        term_pool = ctx.enter_context(tc.tile_pool(name="term_pool", bufs=2))
        out_pool = ctx.enter_context(tc.tile_pool(name="out_pool", bufs=2))
        psum_xt = ctx.enter_context(tc.psum_pool(name="psum_xt", bufs=3))
        psum_mx = ctx.enter_context(tc.psum_pool(name="psum_mx", bufs=1))

        ctx.enter_context(tc.manual_schedule())

        ident_f32 = keep.tile([P, P], F32)
        make_identity(nc, ident_f32[:])
        ident_bf16 = keep.tile([P, P], BF16)
        make_identity(nc, ident_bf16[:])
        minus_half = keep.tile([P, 2, ROW_TILES], F32)
        nc.vector.memset(minus_half[:], -0.5)
        param_rows = keep.tile([P, P], BF16)
        nc.vector.memset(param_rows[:], 0.0)
        param = keep.tile([P, P], F32)
        ln_raw = keep.tile([P, 2, NS, LN_SLOT], BF16)
        ln_param = keep.tile([P, 2, PASSES, PACK], F32)
        gate_bias = keep.tile([P, NS], F32)
        diff_bias = keep.tile([P, NS - 1], F32)
        w_raw = keep.tile([P, PASSES, PACK, W_COLS], BF16)
        w_grouped = keep.tile([P, PASSES, W_COLS, PACK], BF16, align_bytes=64)
        w_codes = keep.tile([P, PASSES, W_COLS], U32, align_bytes=64)
        w_scales = keep.tile([P, PASSES, W_COLS], U8, align_bytes=64)

        def load_ln_vectors():
            for s in range(NS):
                count = len(PASSES_OF_STREAM[s]) * PACK
                for j, vec in enumerate((ln_ws[s], ln_bs[s])):
                    nc.sync.dma_start(
                        out=ln_raw[:, j, s, 0:count].rearrange("p (g t) -> p g t", t=PACK),
                        in_=vec.rearrange("(g p t) -> p g t", p=P, t=PACK),
                    )
            for s in range(NS):
                g0 = PASSES_OF_STREAM[s][0]
                g1 = PASSES_OF_STREAM[s][-1] + 1
                nc.scalar.copy(
                    out=ln_param[:, :, g0:g1, :].rearrange("p j g t -> p j (g t)"),
                    in_=ln_raw[:, :, s, 0 : (g1 - g0) * PACK],
                )

        def load_biases():
            for s in range(NS):
                nc.sync.dma_start(
                    out=param_rows[OUT_BIAS_ROW + s : OUT_BIAS_ROW + s + 1, :],
                    in_=bs[s].rearrange("(c p) -> c p", p=P),
                )
                nc.sync.dma_start(
                    out=param_rows[GATE_BIAS_ROW + NS * s : GATE_BIAS_ROW + NS * (s + 1), :],
                    in_=bgs[s].rearrange("(c p) -> c p", p=P),
                )

        def prepare_biases():
            param_ps = psum_xt.tile([P, P], BF16, tag="xt")
            nc.tensor.transpose(param_ps[:], param_rows[:], ident_bf16[:])
            nc.scalar.copy(out=param[:], in_=param_ps[:])
            nc.gpsimd.tensor_add(
                out=gate_bias[:],
                in0=param[:, GATE_BIAS_ROW : GATE_BIAS_ROW + NS],
                in1=param[:, GATE_BIAS_ROW + NS : GATE_BIAS_ROW + 2 * NS],
            )
            nc.gpsimd.tensor_add(
                out=gate_bias[:],
                in0=gate_bias[:],
                in1=param[:, GATE_BIAS_ROW + 2 * NS : GATE_BIAS_ROW + 3 * NS],
            )
            for i in range(NS - 1):
                nc.gpsimd.tensor_sub(
                    out=diff_bias[:, i : i + 1], in0=gate_bias[:, i : i + 1],
                    in1=gate_bias[:, NS - 1 : NS],
                )

        def load_weights(g):
            s = STREAM_OF_PASS[g]
            r0 = (g - PASSES_OF_STREAM[s][0]) * K_PASS
            rows = slice(r0, r0 + K_PASS)
            nc.sync.dma_start(
                out=w_raw[:, g, :, 0:OUT],
                in_=Ws[s][rows, :].rearrange("(p t) n -> p t n", t=PACK),
            )
            nc.sync.dma_start(
                out=w_raw[:, g, :, OUT:W_COLS],
                in_=Wgs[s][rows, :].rearrange("(p t) n -> p t n", t=PACK),
            )

        def regroup_weights(g):
            for c0, c1, sign in ((0, LAST_GATE_COL, 1.0), (LAST_GATE_COL, W_COLS, -1.0)):
                nc.scalar.activation(
                    out=w_grouped[:, g, c0:c1, :].rearrange("p (c i) t -> p c t i", i=4),
                    in_=w_raw[:, g, :, c0:c1].rearrange("p t (c i) -> p c t i", i=4),
                    func=ACT.Copy, scale=sign,
                )

        def quantise_weights(g):
            nc.vector.quantize_mx(
                out=w_codes[:, g, :].bitcast(FP8X4),
                scales=w_scales[:, g, :],
                in_=w_grouped[:, g, :, :].rearrange("p n t -> p (n t)"),
            )

        x_blks = {}
        partials = {}
        mean_vars = {}
        rstds = {}
        var_epses = {}
        late_shifts = {}
        shifts = {}
        x_norms = {}
        planes_of = {}
        grouped_of = {}
        f_codes_of = {}
        f_scales_of = {}
        terms_of = {}
        gate = {}

        def load(b):
            x_blks[b] = x_pool.tile([P, ROW_TILES, K_ALL], BF16, name="x_blk")
            rows = slice(b * BLOCK, (b + 1) * BLOCK)
            for s in range(NS):
                k0 = PASSES_OF_STREAM[s][0] * K_PASS
                k1 = (PASSES_OF_STREAM[s][-1] + 1) * K_PASS
                nc.sync.dma_start(
                    out=x_blks[b][:, :, k0:k1],
                    in_=xs[s][rows, :].rearrange("(p t) k -> p t k", t=ROW_TILES),
                )

        def statistics(b, g):
            if g == 0:
                partials[b] = stat_pool.tile([P, ROW_TILES, PASSES, 6], F32, name="partial")
            for t in range(ROW_TILES):
                nc.vector.bn_stats(
                    out=partials[b][:, t, g, :], in_=x_blks[b][:, t, g * K_PASS : (g + 1) * K_PASS]
                )
            if g % 2 == 1:
                h = g // 2
                count = len(STREAMS_OF_HALF[h])
                mean_vars[b, h] = stat_pool.tile([P, count, ROW_TILES, 2], F32, name="mean_var")
                for k, s in enumerate(STREAMS_OF_HALF[h]):
                    g0 = PASSES_OF_STREAM[s][0]
                    g1 = PASSES_OF_STREAM[s][-1] + 1
                    for t in range(ROW_TILES):
                        nc.vector.bn_aggr(
                            out=mean_vars[b, h][:, k, t, :],
                            in_=partials[b][:, t, g0:g1, :].rearrange("p g v -> p (g v)"),
                        )

        def add_epsilon(b, h):
            count = len(STREAMS_OF_HALF[h])
            var_epses[b, h] = stat_pool.tile([P, count, ROW_TILES], F32, name="var_eps")
            nc.vector.tensor_scalar_add(
                out=var_epses[b, h][:], in0=mean_vars[b, h][:, :, :, 1], scalar1=EPS
            )

        def inverse_deviation(b, h):
            count = len(STREAMS_OF_HALF[h])
            rstds[b, h] = stat_pool.tile([P, count, ROW_TILES], F32, name="rstd")
            nc.gpsimd.tensor_tensor(
                out=rstds[b, h][:], in0=var_epses[b, h][:], in1=minus_half[:, 0:count, :], op=ALU.pow
            )

        def normalise(i, engines):
            b, g = divmod(i, PASSES)
            h = g // 2
            k = STREAMS_OF_HALF[h].index(STREAM_OF_PASS[g])
            if "gpsimd" in engines:
                late_shifts[i] = stat_pool.tile([P, ROW_TILES], F32, name="late_shift")
                nc.vector.scalar_tensor_tensor(
                    out=late_shifts[i][:], in0=mean_vars[b, h][:, k, :, 0], scalar=-1.0,
                    in1=rstds[b, h][:, k, :], op0=ALU.mult, op1=ALU.mult,
                )
                x_norms[i] = norm_pool.tile([P, ROW_TILES, PACK, P], F32, name="x_norm")
            late_shift = late_shifts[i]
            for t in range(ROW_TILES):
                if norm_engine(i, t) not in engines:
                    continue
                x_rows = x_blks[b][:, t, g * K_PASS : (g + 1) * K_PASS].rearrange(
                    "p (h i j) -> p h j i", i=4, j=PACK
                )
                normed = x_norms[i][:, t, :, :].rearrange("p j (h i) -> p h j i", i=4)
                scale = rstds[b, h][:, k, t : t + 1]
                bias = late_shift[:, t : t + 1]
                if norm_engine(i, t) == "scalar":
                    nc.scalar.activation(
                        out=normed, in_=x_rows, func=ACT.Identity, scale=scale, bias=bias
                    )
                elif norm_engine(i, t) == "vector":
                    nc.vector.tensor_scalar(
                        out=normed, in0=x_rows, scalar1=scale, scalar2=bias, op0=ALU.mult, op1=ALU.add
                    )
                else:
                    nc.gpsimd.tensor_scalar(
                        out=normed, in0=x_rows, scalar1=scale, scalar2=late_shift[:, t : t + 1],
                        op0=ALU.mult, op1=ALU.add,
                    )

        def transpose_and_scale(i):
            g = i % PASSES
            planes_of[i] = plane_pool.tile([P, PACK, BLOCK], BF16, name="planes")
            for j in range(PACK):
                x_t = psum_xt.tile([P, BLOCK], F32, tag="xt")
                for t in range(ROW_TILES):
                    nc.tensor.transpose(
                        x_t[:, t * P : (t + 1) * P], x_norms[i][:, t, j, :], ident_f32[:]
                    )
                gain = ln_param[:, 0, g, j : j + 1]
                offset = ln_param[:, 1, g, j : j + 1]
                if copy_engine(i, j) == "scalar":
                    nc.scalar.activation(
                        out=planes_of[i][:, j, :], in_=x_t[:], func=ACT.Relu, scale=gain, bias=offset
                    )
                else:
                    nc.vector.tensor_scalar(
                        out=planes_of[i][:, j, :], in0=x_t[:], scalar1=gain, scalar2=offset,
                        op0=ALU.mult, op1=ALU.add,
                    )

        def regroup_features(i):
            grouped_of[i] = f_pool.tile([P, BLOCK, PACK], BF16, name="grouped", align_bytes=64)
            grouped = grouped_of[i][:].rearrange("p (c i) t -> p c t i", i=4)
            planes = planes_of[i][:].rearrange("p t (c i) -> p c t i", i=4)
            if regroup_engine(i) == "scalar":
                nc.scalar.activation(out=grouped, in_=planes, func=ACT.Relu)
            else:
                nc.vector.tensor_scalar_max(out=grouped, in0=planes, scalar1=0.0)

        def quantise_features(i):
            b, g = divmod(i, PASSES)
            if g == 0:
                f_codes_of[b] = code_pool.tile([P, PASSES, BLOCK], U32, name="f_codes", align_bytes=64)
                f_scales_of[b] = code_pool.tile([P, PASSES, BLOCK], U8, name="f_scales", align_bytes=64)
            nc.vector.quantize_mx(
                out=f_codes_of[b][:, g, :].bitcast(FP8X4),
                scales=f_scales_of[b][:, g, :],
                in_=grouped_of[i][:].rearrange("p r t -> p (r t)"),
            )

        def product(acc, b, g, c, start, stop):
            nc.tensor.matmul_mx(
                out=acc[:],
                lhsT=w_codes[:, g, c : c + P].bitcast(FP8X4), lhsT_scale=w_scales[:, g, c : c + P],
                rhs=f_codes_of[b][:, g, :].bitcast(FP8X4), rhs_scale=f_scales_of[b][:, g, :],
                start=start, stop=stop,
            )

        def sum_transposed(acc, terms):
            for t in range(ROW_TILES):
                for i in range(NS):
                    nc.tensor.matmul(
                        out=acc[:, t * P : (t + 1) * P], lhsT=terms[i][:, t * P : (t + 1) * P],
                        rhs=ident_f32[:], is_transpose=True, start=(i == 0), stop=(i == NS - 1),
                    )

        def gate_tile(name):
            gate[name] = gate_pool.tile([P, BLOCK], F32, name=name)
            return gate[name]

        def term_tile(b, name):
            terms_of[b, name] = term_pool.tile([P, BLOCK], F32, name=name)
            return terms_of[b, name]

        def logit_differences(b, passes):
            for i in range(NS - 1):
                if 0 in passes:
                    gate["diff%d" % i] = psum_mx.tile([P, BLOCK], F32, name="diff%d" % i)
                for g in passes:
                    product(gate["diff%d" % i], b, g, OUT + i * OUT, g == 0, False)
                    product(gate["diff%d" % i], b, g, LAST_GATE_COL, False, g == PASSES - 1)

        def maximum_with_zero(b):
            nc.scalar.activation(
                out=gate_tile("top02")[:], in_=gate["diff0"][:], func=ACT.Relu,
                bias=diff_bias[:, 0:1], scale=1.0,
            )

        def maximum(b):
            nc.vector.scalar_tensor_tensor(
                out=gate_tile("top")[:], in0=gate["diff1"][:], scalar=diff_bias[:, 1:2],
                in1=gate["top02"][:], op0=ALU.add, op1=ALU.max,
            )

        def take_off_maximum(b):
            for i in range(NS - 1):
                nc.vector.scalar_tensor_tensor(
                    out=gate_tile("below%d" % i)[:], in0=gate["diff%d" % i][:],
                    scalar=diff_bias[:, i : i + 1], in1=gate["top"][:], op0=ALU.add, op1=ALU.subtract,
                )

        def exponentials(b):
            nc.scalar.activation(
                out=term_tile(b, "expo%d" % (NS - 1))[:], in_=gate["top"][:], func=ACT.Exp, scale=-1.0
            )
            for i in range(NS - 1):
                nc.scalar.activation(
                    out=term_tile(b, "expo%d" % i)[:], in_=gate["below%d" % i][:], func=ACT.Exp
                )

        def stream_products(b):
            for s in range(NS):
                gate["y%d" % s] = psum_mx.tile([P, BLOCK], F32, name="y%d" % s, tag="y%d" % s)
                passes = PASSES_OF_STREAM[s]
                for g in passes:
                    product(gate["y%d" % s], b, g, 0, g == passes[0], g == passes[-1])

        def weigh(b):
            for s in (NS - 1, *range(NS - 1)):
                nc.vector.scalar_tensor_tensor(
                    out=term_tile(b, "weighted%d" % s)[:], in0=gate["y%d" % s][:],
                    scalar=param[:, OUT_BIAS_ROW + s : OUT_BIAS_ROW + s + 1],
                    in1=terms_of[b, "expo%d" % s][:], op0=ALU.add, op1=ALU.mult,
                )

        def denominator(b, pool, tag):
            terms_of[b, "denom"] = pool.tile([P, BLOCK], F32, name="denom", tag=tag)
            sum_transposed(terms_of[b, "denom"], [terms_of[b, "expo%d" % i] for i in range(NS)])

        def log_denominator(b):
            nc.scalar.activation(
                out=term_tile(b, "log_denom")[:], in_=terms_of[b, "denom"][:], func=ACT.Ln
            )

        def invert(b):
            nc.scalar.activation(
                out=term_tile(b, "inverse")[:], in_=terms_of[b, "log_denom"][:], func=ACT.Exp, scale=-1.0
            )

        def numerator(b, pool, tag):
            terms_of[b, "numer"] = pool.tile([P, BLOCK], F32, name="numer", tag=tag)
            sum_transposed(terms_of[b, "numer"], [terms_of[b, "weighted%d" % s] for s in range(NS)])

        def finish(b):
            merged = out_pool.tile([P, BLOCK], F32)
            nc.vector.tensor_mul(
                out=merged[:], in0=terms_of[b, "numer"][:], in1=terms_of[b, "inverse"][:]
            )
            nc.sync.dma_start(
                out=out[b * BLOCK : (b + 1) * BLOCK, :].rearrange("(p t) n -> p (t n)", t=ROW_TILES),
                in_=merged[:],
            )

        group_of_last = {group[-1]: group for group in GROUPS}

        def merge_step(b, offset):
            return b * PASSES + offset - (TAIL_GAIN if b == N_BLOCKS - 1 else 0)

        def weighed(i, offset):
            return tuple(
                b for b in range(N_BLOCKS) if merge_step(b, offset) + (1 if b == N_BLOCKS - 2 else 0) == i
            )

        def lag_of(k, lag):
            return 1 if k >= N_ITEMS - PASSES else lag

        def items_due(i, lag):
            return [k for k in range(N_ITEMS) if k + lag_of(k, lag) == i]

        def step(i):
            def merging(offset):
                return tuple(b for b in range(N_BLOCKS) if merge_step(b, offset) == i)

            def ending(offset):
                return [b for last in merging(offset) for b in group_of_last.get(last, ())]

            def is_item(n):
                return 0 <= n < N_ITEMS

            def half_ends(n):
                b, g = divmod(n, PASSES)
                return ((b, g // 2),) if is_item(n) and g % 2 == 1 else ()

            for b, h in half_ends(i + RSTD_LEAD):
                add_epsilon(b, h)
            for b in merging(BELOW_STEP):
                take_off_maximum(b)
            for b in ending(FINISH_STEP):
                finish(b)
            for b in range(N_BLOCKS):
                passes = (LAST_LOGIT_STEPS if b == N_BLOCKS - 1 else LOGIT_STEPS).get(i - b * PASSES, ())
                logit_differences(b, passes)
            for place, b in enumerate(ending(LOG_STEP)):
                if b not in GROUPS[-1]:
                    denominator(b, psum_mx, "y%d" % place)
            for place, b in enumerate(ending(INVERT_STEP)):
                if b not in GROUPS[-1]:
                    numerator(b, psum_mx, "y%d" % place)
            for b in merging(WEIGH_STEP):
                if b == N_BLOCKS - 2:
                    denominator(b, psum_xt, "xt")
            for b in weighed(i, LOG_STEP):
                if b == N_BLOCKS - 2:
                    numerator(b, psum_xt, "xt")
            for b in merging(INVERT_STEP):
                if b == N_BLOCKS - 1:
                    numerator(b, psum_xt, "xt")
            for b in weighed(i, WEIGH_STEP):
                weigh(b)
            for b in weighed(i, EXP_STEP):
                if b < N_BLOCKS - 1:
                    stream_products(b)
            for k in items_due(i, QUANT_LAG):
                if k < N_ITEMS - PASSES:
                    quantise_features(k)
            for k in items_due(i, REGROUP_LAG):
                regroup_features(k)
            for k in items_due(i, QUANT_LAG):
                if k >= N_ITEMS - PASSES:
                    quantise_features(k)
            if is_item(i + NORM_LEAD):
                normalise(i + NORM_LEAD, ("gpsimd", "vector"))
            for b, h in half_ends(i + RSTD_LEAD):
                inverse_deviation(b, h)
            for b in merging(TOP_STEP):
                maximum_with_zero(b)
            for b in merging(EXP_STEP):
                exponentials(b)
                if b == N_BLOCKS - 1:
                    denominator(b, psum_xt, "xt")
                    stream_products(b)
            for b in ending(LOG_STEP):
                log_denominator(b)
            for b in ending(INVERT_STEP):
                invert(b)
            if is_item(i):
                transpose_and_scale(i)
            if is_item(i + NORM_LEAD):
                normalise(i + NORM_LEAD, ("scalar",))
            if is_item(i + STATS_LEAD):
                statistics(*divmod(i + STATS_LEAD, PASSES))
            for b in merging(TOP_STEP):
                maximum(b)
            if i % PASSES == 0 and 1 <= i // PASSES < N_BLOCKS - 2:
                load(i // PASSES + 2)

        load(0)
        load_ln_vectors()
        for g in range(PASSES):
            load_weights(g)
        load(1)
        load_biases()
        load(2)
        for i in range(-STATS_LEAD, N_ITEMS - PASSES + FINISH_STEP - TAIL_GAIN + 1):
            step(i)
            if i == -2:
                regroup_weights(0)
                regroup_weights(1)
            if i == 1:
                regroup_weights(2)
            if i == 2:
                regroup_weights(3)
            if i in range(2, 2 + PASSES):
                quantise_weights(i - 2)
            if i == 5:
                prepare_biases()
